import numpy as np
import ml_dtypes


def mxq(x, axis, fmt="e4m3"):
    dtype, down = {"e4m3": (ml_dtypes.float8_e4m3fn, 7), "e5m2": (ml_dtypes.float8_e5m2, 14)}[fmt]
    v = np.moveaxis(np.asarray(x, np.float32).astype(ml_dtypes.bfloat16).astype(np.float64), axis, -1)
    blocks = v.reshape(v.shape[:-1] + (-1, 32))
    amax = np.abs(blocks).max(-1, keepdims=True)
    byte = np.maximum(np.where(amax > 0, np.frexp(amax)[1] - 1 + 127, 0) - down, 1)
    scale = np.exp2(byte - 127.0)
    codes = (blocks / scale).astype(np.float32).astype(dtype).astype(np.float64)
    return np.moveaxis((codes * scale).reshape(v.shape), -1, axis)


WIDE = False


def mx_kscale(k):
    if not WIDE:
        return np.ones(k)
    levels = np.array([10, -10, 5, -5, 0])
    if k % 512:
        return np.exp2(np.random.permutation(np.resize(levels, k // 32))).repeat(32)
    a = np.empty((k // 512, 16))
    for p in range(k // 512):
        a[p, :8] = np.random.permutation(np.resize(levels, 8))
        for g in range(8):
            far = levels[np.abs(levels - a[p, g]) >= 10]
            a[p, g + 8] = far[np.random.randint(len(far))]
    return np.exp2(a.ravel()).repeat(32)


BF16 = ml_dtypes.bfloat16


def bf(x):
    return np.asarray(x, np.float32).astype(BF16)


def f64(x):
    return np.asarray(x).astype(np.float64)


N, D_FEAT, D_EMB, H = 16, 511, 512, 4
SEQ = D_FEAT + 1
EPS = 1e-5


def ln(x):
    m = x.mean(-1, keepdims=True)
    v = ((x - m) ** 2).mean(-1, keepdims=True)
    return (x - m) / np.sqrt(v + EPS)


def setup_inputs():
    s = mx_kscale(D_EMB)
    return {'Z': bf(0.5 + 1.5 * np.random.standard_normal((N, D_FEAT))),
            'feat_emb': bf(np.random.standard_normal((D_FEAT, D_EMB)) * 0.02 + 0.01),
            'label_token': bf(np.random.standard_normal((1, 1, D_EMB)) * 0.02 + 0.01),
            'g1': bf((1.0 + 0.1 * np.random.standard_normal(D_EMB)) * s),
            'be1': bf(0.1 * np.random.standard_normal(D_EMB) * s),
            'wk': bf(np.random.standard_normal((D_EMB, D_EMB)) / np.sqrt(D_EMB) / s[:, None]),
            'bk': bf(0.3 * np.random.standard_normal(D_EMB)),
            'wv': bf(np.random.standard_normal((D_EMB, D_EMB)) / np.sqrt(D_EMB) / s[:, None]),
            'bv': bf(0.3 * np.random.standard_normal(D_EMB))}


def reference(Z, feat_emb, label_token, g1, be1, wk, bk, wv, bv):
    n = Z.shape[0]
    zn = ln(f64(Z))
    x_feats = zn[..., None] * f64(feat_emb)[None]
    lab = np.broadcast_to(f64(label_token), (n, 1, D_EMB))
    x = np.concatenate([x_feats, lab], axis=1)
    xn = ln(x) * f64(g1) + f64(be1)
    xq = mxq(xn, 2, 'e4m3')
    k = (xq @ mxq(f64(wk), 0, 'e4m3')) + f64(bk)
    v = (xq @ mxq(f64(wv), 0, 'e4m3')) + f64(bv)
    return k, v

@@ -1,0 +1,283 @@
+from contextlib import ExitStack
+
+import concourse.mybir as mybir
+from concourse.masks import make_identity
+
+F32 = mybir.dt.float32
+BF16 = mybir.dt.bfloat16
+U32 = mybir.dt.uint32
+U8 = mybir.dt.uint8
+FP8X4 = mybir.dt.float8_e4m3fn_x4
+ALU = mybir.AluOpType
+ACT = mybir.ActivationFunctionType
+
+P = 128
+PACK = 4
+N_B = 16
+D_FEAT = 511
+SEQ = 512
+D_EMB = 512
+TILES = SEQ // P
+EPS = 1e-5
+QUANT_AFTER = 6
+
+FLOPS = 2 * N_B * SEQ * D_EMB * (2 * D_EMB)
+
+
+def tile_causalfeaturetransformer_pa_t_kernel(
+    tc, Z, feat_emb, label_token, g1, be1, wk, bk, wv, bv, out_0, out_1
+):
+    nc = tc.nc
+    weights = (wk, wv)
+    biases = (bk, bv)
+    out_views = tuple(o.rearrange("n (p j) e -> n p j e", j=TILES) for o in (out_0, out_1))
+
+    with ExitStack() as ctx:
+        ctx.enter_context(tc.manual_schedule())
+        keep = ctx.enter_context(tc.tile_pool(name="keep", bufs=1))
+        work = ctx.enter_context(tc.tile_pool(name="work", bufs=2))
+        results = ctx.enter_context(tc.tile_pool(name="results", bufs=3))
+        psum_t = ctx.enter_context(tc.psum_pool(name="psum_t", bufs=4))
+        psum_mx = ctx.enter_context(tc.psum_pool(name="psum_mx", bufs=4))
+
+        one_col = keep.tile([P, 1], F32)
+        nc.vector.memset(one_col[:], 1.0)
+        warm = keep.tile([P, 1], F32)
+        nc.scalar.activation(out=warm[:], in_=one_col[:], func=ACT.Sqrt)
+        ident_f32 = keep.tile([P, P], F32)
+        make_identity(nc, ident_f32[:])
+
+        z_raw = keep.tile([N_B, SEQ], BF16)
+        nc.vector.memset(z_raw[:], 0.0)
+        nc.sync.dma_start(out=z_raw[:, 0:D_FEAT], in_=Z)
+
+        tokens = keep.tile([P, TILES, D_EMB], BF16)
+        nc.sync.dma_start(
+            out=tokens[0:112], in_=feat_emb[0:448].rearrange("(p j) d -> p j d", j=TILES)
+        )
+        nc.sync.dma_start(
+            out=tokens[112:127], in_=feat_emb[448:508].rearrange("(p j) d -> p j d", j=TILES)
+        )
+        nc.sync.dma_start(
+            out=tokens[127:128, 0:3, :], in_=feat_emb[508:511].rearrange("(p j) d -> p j d", p=1)
+        )
+        nc.sync.dma_start(out=tokens[127:128, 3:4, :], in_=label_token)
+
+        gain_raw = keep.tile([P, PACK], BF16)
+        nc.scalar.dma_start(out=gain_raw[:], in_=g1.rearrange("(q t) -> q t", t=PACK))
+        shift_raw = keep.tile([P, PACK], BF16)
+        nc.scalar.dma_start(out=shift_raw[:], in_=be1.rearrange("(q t) -> q t", t=PACK))
+
+        w_raw = []
+        for o in range(2):
+            raw = keep.tile([P, PACK, D_EMB], BF16, name="w_raw%d" % o)
+            nc.sync.dma_start(out=raw[:], in_=weights[o].rearrange("(q t) e -> q t e", t=PACK))
+            w_raw.append(raw)
+
+        bias_all = keep.tile([P, 2, D_EMB], BF16)
+        for o in range(2):
+            nc.scalar.dma_start(out=bias_all[:, o, :], in_=biases[o].partition_broadcast(P))
+
+        zn_rows = keep.tile([P, SEQ], F32)
+        nc.vector.memset(zn_rows[:], 0.0)
+
+        z_stats = keep.tile([N_B, 6], F32)
+        nc.vector.bn_stats(out=z_stats[:], in_=z_raw[:, 0:D_FEAT])
+        z_mv = keep.tile([N_B, 2], F32)
+        nc.vector.bn_aggr(out=z_mv[:], in_=z_stats[:])
+        z_var_eps = keep.tile([N_B, 1], F32)
+        nc.vector.tensor_scalar(
+            out=z_var_eps[:], in0=z_mv[:, 1:2], scalar1=EPS, scalar2=None, op0=ALU.add
+        )
+        z_sd = keep.tile([N_B, 1], F32)
+        nc.scalar.activation(out=z_sd[:], in_=z_var_eps[:], func=ACT.Sqrt)
+        z_rstd = keep.tile([N_B, 1], F32)
+        nc.vector.reciprocal(out=z_rstd[:], in_=z_sd[:])
+        nc.vector.tensor_scalar(
+            out=zn_rows[0:N_B, :].rearrange("n (j p) -> n j p", j=TILES),
+            in0=z_raw[:].rearrange("n (p j) -> n j p", j=TILES),
+            scalar1=z_mv[:, 0:1],
+            scalar2=z_rstd[:],
+            op0=ALU.subtract,
+            op1=ALU.mult,
+        )
+        nc.vector.memset(zn_rows[0:N_B, SEQ - 1 : SEQ], 1.0)
+        zn_psum = psum_t.tile([P, TILES, P], F32, tag="t")
+        for j in range(TILES):
+            nc.tensor.transpose(zn_psum[:, j, :], zn_rows[:, j * P : (j + 1) * P], ident_f32[:])
+
+        tokens_split = keep.tile([P, TILES, PACK, P], BF16)
+        for j in range(TILES):
+            nc.scalar.copy(
+                out=tokens_split[:, j, :, :],
+                in_=tokens[:, j, :].rearrange("p (q t) -> p t q", t=PACK),
+            )
+
+        tok_stats = keep.tile([P, TILES, 6], F32)
+        tok_mv = keep.tile([P, TILES, 2], F32)
+        for j in range(TILES):
+            nc.vector.bn_stats(out=tok_stats[:, j, :], in_=tokens[:, j, :])
+            nc.vector.bn_aggr(out=tok_mv[:, j, :], in_=tok_stats[:, j, :])
+        neg_mean = keep.tile([P, TILES, 1], F32)
+        nc.vector.tensor_scalar(
+            out=neg_mean[:], in0=tok_mv[:, :, 0:1], scalar1=-1.0, scalar2=None, op0=ALU.mult
+        )
+
+        shape_c = [P, TILES, N_B]
+        zn_cols = keep.tile(shape_c, F32)
+        nc.vector.tensor_copy(out=zn_cols[:], in_=zn_psum[:, :, 0:N_B])
+        zn_sq = keep.tile(shape_c, F32)
+        nc.vector.tensor_tensor(out=zn_sq[:], in0=zn_cols[:], in1=zn_cols[:], op=ALU.mult)
+        x_var = keep.tile(shape_c, F32)
+        nc.vector.tensor_tensor(
+            out=x_var[:], in0=zn_sq[:], in1=tok_mv[:, :, 1:2].to_broadcast(shape_c), op=ALU.mult
+        )
+        x_var_eps = keep.tile(shape_c, F32)
+        nc.vector.tensor_scalar(
+            out=x_var_eps[:], in0=x_var[:], scalar1=EPS, scalar2=None, op0=ALU.add
+        )
+        x_sd = keep.tile(shape_c, F32)
+        nc.scalar.activation(out=x_sd[:], in_=x_var_eps[:], func=ACT.Sqrt)
+        x_rstd = keep.tile(shape_c, F32)
+        nc.vector.reciprocal(out=x_rstd[:], in_=x_sd[:])
+        c_scale = keep.tile(shape_c, F32)
+        nc.vector.tensor_tensor(out=c_scale[:], in0=zn_cols[:], in1=x_rstd[:], op=ALU.mult)
+        c_shift = keep.tile(shape_c, F32)
+        nc.vector.tensor_tensor(
+            out=c_shift[:], in0=c_scale[:], in1=neg_mean[:].to_broadcast(shape_c), op=ALU.mult
+        )
+        gain_cols = keep.tile([P, 2 * PACK], F32)
+        nc.vector.tensor_copy(out=gain_cols[:, 0:PACK], in_=gain_raw[:])
+        nc.vector.tensor_copy(out=gain_cols[:, PACK : 2 * PACK], in_=shift_raw[:])
+
+        w_grouped = []
+        for o in range(2):
+            grouped_w = keep.tile([P, D_EMB, PACK], BF16, name="w_grouped%d" % o, align_bytes=64)
+            nc.gpsimd.tensor_scalar(
+                out=grouped_w[:],
+                in0=w_raw[o][:].rearrange("q t e -> q e t"),
+                scalar1=1.0,
+                scalar2=0.0,
+                op0=ALU.mult,
+                op1=ALU.add,
+            )
+            w_grouped.append(grouped_w)
+        w_codes = []
+        w_scales = []
+
+        def quantise_weights():
+            for o in range(2):
+                codes_w = keep.tile([P, D_EMB], U32, name="w_codes%d" % o, align_bytes=64)
+                scales_w = keep.tile([P, D_EMB], U8, name="w_scales%d" % o, align_bytes=64)
+                nc.vector.quantize_mx(
+                    out=codes_w[:].bitcast(FP8X4),
+                    scales=scales_w[:],
+                    in_=w_grouped[o][:].rearrange("q e t -> q (e t)"),
+                )
+                w_codes.append(codes_w)
+                w_scales.append(scales_w)
+
+        z_of = {}
+        grouped_of = {}
+        codes_of = {}
+
+        def scale_rows(n, on_vector=False):
+            z = work.tile([P, TILES, D_EMB], F32, name="z")
+            for j in range(TILES):
+                if on_vector:
+                    nc.vector.tensor_scalar(
+                        out=z[:, j, :],
+                        in0=tokens_split[:, j, :, :].rearrange("p t q -> p (t q)"),
+                        scalar1=c_scale[:, j, n : n + 1],
+                        scalar2=c_shift[:, j, n : n + 1],
+                        op0=ALU.mult,
+                        op1=ALU.add,
+                    )
+                else:
+                    nc.scalar.activation(
+                        out=z[:, j, :],
+                        in_=tokens_split[:, j, :, :].rearrange("p t q -> p (t q)"),
+                        func=ACT.Identity,
+                        scale=c_scale[:, j, n : n + 1],
+                        bias=c_shift[:, j, n : n + 1],
+                    )
+            z_of[n] = z
+
+        def normalise(n):
+            z = z_of[n]
+            planes = work.tile([P, PACK, SEQ], BF16, name="planes")
+            for t in range(PACK):
+                z_t = psum_t.tile([P, SEQ], F32, tag="t")
+                for j in range(TILES):
+                    nc.tensor.transpose(
+                        z_t[:, j * P : (j + 1) * P], z[:, j, t * P : (t + 1) * P], ident_f32[:]
+                    )
+                nc.scalar.activation(
+                    out=planes[:, t, :],
+                    in_=z_t[:],
+                    func=ACT.Identity,
+                    scale=gain_cols[:, t : t + 1],
+                    bias=gain_cols[:, PACK + t : PACK + t + 1],
+                )
+            grouped = work.tile([P, SEQ, PACK], BF16, name="grouped", align_bytes=64)
+            nc.gpsimd.tensor_scalar(
+                out=grouped[:],
+                in0=planes[:].rearrange("q t w -> q w t"),
+                scalar1=1.0,
+                scalar2=0.0,
+                op0=ALU.mult,
+                op1=ALU.add,
+            )
+            grouped_of[n] = grouped
+
+        def quantise(n):
+            codes = work.tile([P, SEQ], U32, name="codes", align_bytes=64)
+            scales = work.tile([P, SEQ], U8, name="scales", align_bytes=64)
+            nc.vector.quantize_mx(
+                out=codes[:].bitcast(FP8X4),
+                scales=scales[:],
+                in_=grouped_of[n][:].rearrange("q w t -> q (w t)"),
+            )
+            codes_of[n] = (codes, scales)
+
+        def project(n):
+            codes, scales = codes_of[n]
+            res = [results.tile([P, TILES, D_EMB], F32, name="res%d" % o) for o in range(2)]
+            for j in range(TILES):
+                cols = slice(j * P, (j + 1) * P)
+                for o in range(2):
+                    if 2 * j + o == QUANT_AFTER and n + 1 < N_B:
+                        quantise(n + 1)
+                    acc = psum_mx.tile([P, D_EMB], F32, name="acc")
+                    nc.tensor.matmul_mx(
+                        out=acc[:],
+                        lhsT=codes[:, cols].bitcast(FP8X4),
+                        lhsT_scale=scales[:, cols],
+                        rhs=w_codes[o][:].bitcast(FP8X4),
+                        rhs_scale=w_scales[o][:],
+                        start=True,
+                        stop=True,
+                    )
+                    nc.vector.tensor_tensor(
+                        out=res[o][:, j, :], in0=acc[:], in1=bias_all[:, o, :], op=ALU.add
+                    )
+                if j % 2 == 1:
+                    for o in range(2):
+                        nc.sync.dma_start(
+                            out=out_views[o][n][:, j - 1 : j + 1, :], in_=res[o][:, j - 1 : j + 1, :]
+                        )
+
+        scale_rows(0)
+        scale_rows(1, on_vector=True)
+        quantise_weights()
+        normalise(0)
+        scale_rows(2)
+        normalise(1)
+        scale_rows(3)
+        quantise(0)
+        for n in range(N_B):
+            project(n)
+            if n + 2 < N_B:
+                normalise(n + 2)
+            if n + 4 < N_B:
+                scale_rows(n + 4)

@@ -40,17 +40,8 @@ def tile_causalfeaturetransformer_pa_t_kernel(
         psum_t = ctx.enter_context(tc.psum_pool(name="psum_t", bufs=4))
         psum_mx = ctx.enter_context(tc.psum_pool(name="psum_mx", bufs=4))
 
-        one_col = keep.tile([P, 1], F32)
-        nc.vector.memset(one_col[:], 1.0)
-        warm = keep.tile([P, 1], F32)
-        nc.scalar.activation(out=warm[:], in_=one_col[:], func=ACT.Sqrt)
-        ident_f32 = keep.tile([P, P], F32)
-        make_identity(nc, ident_f32[:])
-
-        z_raw = keep.tile([N_B, SEQ], BF16)
-        nc.vector.memset(z_raw[:], 0.0)
-        nc.sync.dma_start(out=z_raw[:, 0:D_FEAT], in_=Z)
-
+        z_raw = keep.tile([N_B, D_FEAT], BF16)
+        nc.sync.dma_start(out=z_raw[:], in_=Z)
         tokens = keep.tile([P, TILES, D_EMB], BF16)
         nc.sync.dma_start(
             out=tokens[0:112], in_=feat_emb[0:448].rearrange("(p j) d -> p j d", j=TILES)
@@ -62,66 +53,91 @@ def tile_causalfeaturetransformer_pa_t_kernel(
             out=tokens[127:128, 0:3, :], in_=feat_emb[508:511].rearrange("(p j) d -> p j d", p=1)
         )
         nc.sync.dma_start(out=tokens[127:128, 3:4, :], in_=label_token)
-
-        gain_raw = keep.tile([P, PACK], BF16)
-        nc.scalar.dma_start(out=gain_raw[:], in_=g1.rearrange("(q t) -> q t", t=PACK))
-        shift_raw = keep.tile([P, PACK], BF16)
-        nc.scalar.dma_start(out=shift_raw[:], in_=be1.rearrange("(q t) -> q t", t=PACK))
-
+        gain_rows = keep.tile([P, 2, D_EMB], BF16)
+        nc.vector.memset(gain_rows[:], 0.0)
+        for k, vec in enumerate((g1, be1)):
+            nc.sync.dma_start(out=gain_rows[0:1, k, :], in_=vec.rearrange("(o d) -> o d", o=1))
         w_raw = []
         for o in range(2):
             raw = keep.tile([P, PACK, D_EMB], BF16, name="w_raw%d" % o)
             nc.sync.dma_start(out=raw[:], in_=weights[o].rearrange("(q t) e -> q t e", t=PACK))
             w_raw.append(raw)
-
         bias_all = keep.tile([P, 2, D_EMB], BF16)
         for o in range(2):
-            nc.scalar.dma_start(out=bias_all[:, o, :], in_=biases[o].partition_broadcast(P))
+            nc.sync.dma_start(out=bias_all[:, o, :], in_=biases[o].partition_broadcast(P))
 
+        one_col = keep.tile([P, 1], F32)
+        nc.vector.memset(one_col[:], 1.0)
+        warm = keep.tile([P, 1], F32)
+        nc.scalar.activation(out=warm[:], in_=one_col[:], func=ACT.Sqrt)
+        eps_col = keep.tile([P, 1], F32)
+        nc.vector.tensor_scalar(
+            out=eps_col[:], in0=one_col[:], scalar1=0.0, scalar2=EPS, op0=ALU.mult, op1=ALU.add
+        )
+        ones = keep.tile([P, P], BF16)
+        nc.vector.memset(ones[:], 1.0)
+        ident_f32 = keep.tile([P, P], F32)
+        make_identity(nc, ident_f32[:])
         zn_rows = keep.tile([P, SEQ], F32)
         nc.vector.memset(zn_rows[:], 0.0)
+        nc.vector.memset(zn_rows[0:N_B, SEQ - 1 : SEQ], 1.0)
 
         z_stats = keep.tile([N_B, 6], F32)
-        nc.vector.bn_stats(out=z_stats[:], in_=z_raw[:, 0:D_FEAT])
+        nc.vector.bn_stats(out=z_stats[:], in_=z_raw[:])
         z_mv = keep.tile([N_B, 2], F32)
         nc.vector.bn_aggr(out=z_mv[:], in_=z_stats[:])
-        z_var_eps = keep.tile([N_B, 1], F32)
-        nc.vector.tensor_scalar(
-            out=z_var_eps[:], in0=z_mv[:, 1:2], scalar1=EPS, scalar2=None, op0=ALU.add
-        )
         z_sd = keep.tile([N_B, 1], F32)
-        nc.scalar.activation(out=z_sd[:], in_=z_var_eps[:], func=ACT.Sqrt)
+        nc.scalar.activation(
+            out=z_sd[:], in_=z_mv[:, 1:2], func=ACT.Sqrt, bias=eps_col[0:N_B, :]
+        )
         z_rstd = keep.tile([N_B, 1], F32)
         nc.vector.reciprocal(out=z_rstd[:], in_=z_sd[:])
-        nc.vector.tensor_scalar(
-            out=zn_rows[0:N_B, :].rearrange("n (j p) -> n j p", j=TILES),
-            in0=z_raw[:].rearrange("n (p j) -> n j p", j=TILES),
-            scalar1=z_mv[:, 0:1],
-            scalar2=z_rstd[:],
-            op0=ALU.subtract,
-            op1=ALU.mult,
-        )
-        nc.vector.memset(zn_rows[0:N_B, SEQ - 1 : SEQ], 1.0)
+        zn_view = zn_rows[0:N_B, :].rearrange("n (j p) -> n j p", j=TILES)
+        full = (P - 1) * TILES
+        for dst, cols in (
+            (zn_view[:, :, 0 : P - 1], slice(0, full)),
+            (zn_view[:, 0 : TILES - 1, P - 1 : P], slice(full, D_FEAT)),
+        ):
+            nc.vector.tensor_scalar(
+                out=dst,
+                in0=z_raw[:, cols].rearrange("n (p j) -> n j p", j=dst.shape[1]),
+                scalar1=z_mv[:, 0:1],
+                scalar2=z_rstd[:],
+                op0=ALU.subtract,
+                op1=ALU.mult,
+            )
         zn_psum = psum_t.tile([P, TILES, P], F32, tag="t")
         for j in range(TILES):
             nc.tensor.transpose(zn_psum[:, j, :], zn_rows[:, j * P : (j + 1) * P], ident_f32[:])
 
-        tokens_split = keep.tile([P, TILES, PACK, P], BF16)
-        for j in range(TILES):
-            nc.scalar.copy(
-                out=tokens_split[:, j, :, :],
-                in_=tokens[:, j, :].rearrange("p (q t) -> p t q", t=PACK),
+        spread = []
+        for k in range(2):
+            row_psum = psum_t.tile([P, D_EMB], F32, tag="t")
+            nc.tensor.matmul(
+                out=row_psum[:], lhsT=ones[:], rhs=gain_rows[:, k, :], start=True, stop=True
             )
+            row = keep.tile([P, PACK, P], F32, name="spread%d" % k)
+            nc.scalar.copy(out=row[:], in_=row_psum[:].rearrange("p (q t) -> p t q", t=PACK))
+            spread.append(row)
+        gain, shift = spread
 
         tok_stats = keep.tile([P, TILES, 6], F32)
         tok_mv = keep.tile([P, TILES, 2], F32)
         for j in range(TILES):
             nc.vector.bn_stats(out=tok_stats[:, j, :], in_=tokens[:, j, :])
             nc.vector.bn_aggr(out=tok_mv[:, j, :], in_=tok_stats[:, j, :])
-        neg_mean = keep.tile([P, TILES, 1], F32)
-        nc.vector.tensor_scalar(
-            out=neg_mean[:], in0=tok_mv[:, :, 0:1], scalar1=-1.0, scalar2=None, op0=ALU.mult
-        )
+
+        centred = keep.tile([P, TILES, PACK, P], F32)
+
+        def centre(j):
+            nc.vector.scalar_tensor_tensor(
+                out=centred[:, j, :, :],
+                in0=tokens[:, j, :].rearrange("p (q t) -> p t q", t=PACK),
+                scalar=tok_mv[:, j, 0:1],
+                in1=gain[:],
+                op0=ALU.subtract,
+                op1=ALU.mult,
+            )
 
         shape_c = [P, TILES, N_B]
         zn_cols = keep.tile(shape_c, F32)
@@ -132,152 +148,144 @@ def tile_causalfeaturetransformer_pa_t_kernel(
         nc.vector.tensor_tensor(
             out=x_var[:], in0=zn_sq[:], in1=tok_mv[:, :, 1:2].to_broadcast(shape_c), op=ALU.mult
         )
-        x_var_eps = keep.tile(shape_c, F32)
-        nc.vector.tensor_scalar(
-            out=x_var_eps[:], in0=x_var[:], scalar1=EPS, scalar2=None, op0=ALU.add
-        )
         x_sd = keep.tile(shape_c, F32)
-        nc.scalar.activation(out=x_sd[:], in_=x_var_eps[:], func=ACT.Sqrt)
+        nc.scalar.activation(out=x_sd[:], in_=x_var[:], func=ACT.Sqrt, bias=eps_col[:])
+        centre(0)
         x_rstd = keep.tile(shape_c, F32)
         nc.vector.reciprocal(out=x_rstd[:], in_=x_sd[:])
         c_scale = keep.tile(shape_c, F32)
         nc.vector.tensor_tensor(out=c_scale[:], in0=zn_cols[:], in1=x_rstd[:], op=ALU.mult)
-        c_shift = keep.tile(shape_c, F32)
-        nc.vector.tensor_tensor(
-            out=c_shift[:], in0=c_scale[:], in1=neg_mean[:].to_broadcast(shape_c), op=ALU.mult
+
+        w_grouped = [
+            keep.tile([P, D_EMB, PACK], BF16, name="w_grouped%d" % o, align_bytes=64) for o in range(2)
+        ]
+        nc.gpsimd.tensor_scalar(
+            out=w_grouped[0][:],
+            in0=w_raw[0][:].rearrange("q t e -> q e t"),
+            scalar1=1.0,
+            scalar2=0.0,
+            op0=ALU.mult,
+            op1=ALU.add,
         )
-        gain_cols = keep.tile([P, 2 * PACK], F32)
-        nc.vector.tensor_copy(out=gain_cols[:, 0:PACK], in_=gain_raw[:])
-        nc.vector.tensor_copy(out=gain_cols[:, PACK : 2 * PACK], in_=shift_raw[:])
+        nc.gpsimd.tensor_scalar(
+            out=w_grouped[1][:],
+            in0=w_raw[1][:].rearrange("q t e -> q e t"),
+            scalar1=1.0,
+            scalar2=0.0,
+            op0=ALU.mult,
+            op1=ALU.add,
+        )
+        w_codes = [keep.tile([P, D_EMB], U32, name="w_codes%d" % o, align_bytes=64) for o in range(2)]
+        w_scales = [keep.tile([P, D_EMB], U8, name="w_scales%d" % o, align_bytes=64) for o in range(2)]
 
-        w_grouped = []
-        for o in range(2):
-            grouped_w = keep.tile([P, D_EMB, PACK], BF16, name="w_grouped%d" % o, align_bytes=64)
-            nc.gpsimd.tensor_scalar(
-                out=grouped_w[:],
-                in0=w_raw[o][:].rearrange("q t e -> q e t"),
-                scalar1=1.0,
-                scalar2=0.0,
-                op0=ALU.mult,
-                op1=ALU.add,
+        def quantise_weight(o):
+            nc.vector.quantize_mx(
+                out=w_codes[o][:].bitcast(FP8X4),
+                scales=w_scales[o][:],
+                in_=w_grouped[o][:].rearrange("q e t -> q (e t)"),
             )
-            w_grouped.append(grouped_w)
-        w_codes = []
-        w_scales = []
-
-        def quantise_weights():
-            for o in range(2):
-                codes_w = keep.tile([P, D_EMB], U32, name="w_codes%d" % o, align_bytes=64)
-                scales_w = keep.tile([P, D_EMB], U8, name="w_scales%d" % o, align_bytes=64)
-                nc.vector.quantize_mx(
-                    out=codes_w[:].bitcast(FP8X4),
-                    scales=scales_w[:],
-                    in_=w_grouped[o][:].rearrange("q e t -> q (e t)"),
-                )
-                w_codes.append(codes_w)
-                w_scales.append(scales_w)
 
         z_of = {}
         grouped_of = {}
         codes_of = {}
+        res_of = {}
 
-        def scale_rows(n, on_vector=False):
-            z = work.tile([P, TILES, D_EMB], F32, name="z")
-            for j in range(TILES):
-                if on_vector:
-                    nc.vector.tensor_scalar(
-                        out=z[:, j, :],
-                        in0=tokens_split[:, j, :, :].rearrange("p t q -> p (t q)"),
-                        scalar1=c_scale[:, j, n : n + 1],
-                        scalar2=c_shift[:, j, n : n + 1],
-                        op0=ALU.mult,
-                        op1=ALU.add,
-                    )
-                else:
-                    nc.scalar.activation(
-                        out=z[:, j, :],
-                        in_=tokens_split[:, j, :, :].rearrange("p t q -> p (t q)"),
-                        func=ACT.Identity,
-                        scale=c_scale[:, j, n : n + 1],
-                        bias=c_shift[:, j, n : n + 1],
-                    )
-            z_of[n] = z
+        def scale(n, j, on_vector=False):
+            if j == 0:
+                z_of[n] = work.tile([P, TILES, D_EMB], F32, name="z")
+            dst = z_of[n][:, j, :]
+            src = centred[:, j, :, :].rearrange("p t q -> p (t q)")
+            c = c_scale[:, j, n : n + 1]
+            if on_vector:
+                nc.vector.tensor_scalar(out=dst, in0=src, scalar1=c, scalar2=None, op0=ALU.mult)
+            else:
+                nc.scalar.activation(out=dst, in_=src, func=ACT.Identity, scale=c)
 
-        def normalise(n):
-            z = z_of[n]
-            planes = work.tile([P, PACK, SEQ], BF16, name="planes")
+        def turn(n, j):
+            if j == 0:
+                grouped_of[n] = work.tile([P, SEQ, PACK], BF16, name="grouped", align_bytes=64)
+            xn_t = psum_t.tile([P, PACK, P], F32, tag="t")
             for t in range(PACK):
-                z_t = psum_t.tile([P, SEQ], F32, tag="t")
-                for j in range(TILES):
-                    nc.tensor.transpose(
-                        z_t[:, j * P : (j + 1) * P], z[:, j, t * P : (t + 1) * P], ident_f32[:]
+                for src, first in ((z_of[n][:, j, t * P : (t + 1) * P], True), (shift[:, t, :], False)):
+                    nc.tensor.matmul(
+                        out=xn_t[:, t, :],
+                        lhsT=src,
+                        rhs=ident_f32[:],
+                        start=first,
+                        stop=not first,
+                        is_transpose=True,
                     )
-                nc.scalar.activation(
-                    out=planes[:, t, :],
-                    in_=z_t[:],
-                    func=ACT.Identity,
-                    scale=gain_cols[:, t : t + 1],
-                    bias=gain_cols[:, PACK + t : PACK + t + 1],
+            nc.scalar.copy(
+                out=grouped_of[n][:, j * P : (j + 1) * P, :], in_=xn_t[:].rearrange("q t i -> q i t")
+            )
+
+        def quantise(n, j0, j1):
+            if j0 == 0:
+                codes_of[n] = (
+                    work.tile([P, SEQ], U32, name="codes", align_bytes=64),
+                    work.tile([P, SEQ], U8, name="scales", align_bytes=64),
                 )
-            grouped = work.tile([P, SEQ, PACK], BF16, name="grouped", align_bytes=64)
-            nc.gpsimd.tensor_scalar(
-                out=grouped[:],
-                in0=planes[:].rearrange("q t w -> q w t"),
-                scalar1=1.0,
-                scalar2=0.0,
-                op0=ALU.mult,
-                op1=ALU.add,
-            )
-            grouped_of[n] = grouped
-
-        def quantise(n):
-            codes = work.tile([P, SEQ], U32, name="codes", align_bytes=64)
-            scales = work.tile([P, SEQ], U8, name="scales", align_bytes=64)
-            nc.vector.quantize_mx(
-                out=codes[:].bitcast(FP8X4),
-                scales=scales[:],
-                in_=grouped_of[n][:].rearrange("q w t -> q (w t)"),
-            )
-            codes_of[n] = (codes, scales)
-
-        def project(n):
             codes, scales = codes_of[n]
-            res = [results.tile([P, TILES, D_EMB], F32, name="res%d" % o) for o in range(2)]
-            for j in range(TILES):
-                cols = slice(j * P, (j + 1) * P)
-                for o in range(2):
-                    if 2 * j + o == QUANT_AFTER and n + 1 < N_B:
-                        quantise(n + 1)
-                    acc = psum_mx.tile([P, D_EMB], F32, name="acc")
-                    nc.tensor.matmul_mx(
-                        out=acc[:],
-                        lhsT=codes[:, cols].bitcast(FP8X4),
-                        lhsT_scale=scales[:, cols],
-                        rhs=w_codes[o][:].bitcast(FP8X4),
-                        rhs_scale=w_scales[o][:],
-                        start=True,
-                        stop=True,
-                    )
-                    nc.vector.tensor_tensor(
-                        out=res[o][:, j, :], in0=acc[:], in1=bias_all[:, o, :], op=ALU.add
-                    )
-                if j % 2 == 1:
-                    for o in range(2):
-                        nc.sync.dma_start(
-                            out=out_views[o][n][:, j - 1 : j + 1, :], in_=res[o][:, j - 1 : j + 1, :]
-                        )
+            cols = slice(j0 * P, j1 * P)
+            nc.vector.quantize_mx(
+                out=codes[:, cols].bitcast(FP8X4),
+                scales=scales[:, cols],
+                in_=grouped_of[n][:, cols, :].rearrange("q w t -> q (w t)"),
+            )
 
-        scale_rows(0)
-        scale_rows(1, on_vector=True)
-        quantise_weights()
-        normalise(0)
-        scale_rows(2)
-        normalise(1)
-        scale_rows(3)
-        quantise(0)
+        def project(n, j, o):
+            codes, scales = codes_of[n]
+            if j == 0 and o == 0:
+                res_of[n] = [results.tile([P, TILES, D_EMB], F32, name="res%d" % k) for k in range(2)]
+            cols = slice(j * P, (j + 1) * P)
+            acc = psum_mx.tile([P, D_EMB], F32, name="acc")
+            nc.tensor.matmul_mx(
+                out=acc[:],
+                lhsT=codes[:, cols].bitcast(FP8X4),
+                lhsT_scale=scales[:, cols],
+                rhs=w_codes[o][:].bitcast(FP8X4),
+                rhs_scale=w_scales[o][:],
+                start=True,
+                stop=True,
+            )
+            nc.vector.tensor_tensor(
+                out=res_of[n][o][:, j, :], in0=acc[:], in1=bias_all[:, o, :], op=ALU.add
+            )
+            if j % 2 == 1:
+                nc.sync.dma_start(
+                    out=out_views[o][n][:, j - 1 : j + 1, :], in_=res_of[n][o][:, j - 1 : j + 1, :]
+                )
+
+        for j in range(TILES):
+            if j > 0:
+                centre(j)
+            scale(0, j, on_vector=True)
+            turn(0, j)
+            scale(1, j)
+        quantise_weight(0)
+        quantise_weight(1)
+        quantise(0, 0, 1)
+        for j in range(TILES):
+            if j + 1 < TILES:
+                quantise(0, j + 1, j + 2)
+            else:
+                quantise(1, 0, TILES)
+            for o in range(2):
+                project(0, j, o)
+            if j < 2:
+                for i in (2 * j, 2 * j + 1):
+                    turn(1, i)
+                    scale(2, i)
+
         for n in range(N_B):
-            project(n)
-            if n + 2 < N_B:
-                normalise(n + 2)
-            if n + 4 < N_B:
-                scale_rows(n + 4)
+            for j in range(TILES):
+                if n > 0:
+                    for o in range(2):
+                        if 2 * j + o == QUANT_AFTER and n + 1 < N_B:
+                            quantise(n + 1, 0, TILES)
+                        project(n, j, o)
+                if j % 2 == 1 and n + 2 < N_B:
+                    for i in (j - 1, j):
+                        turn(n + 2, i)
+                        if n + 3 < N_B:
+                            scale(n + 3, i)

@@ -19,7 +19,10 @@ SEQ = 512
 D_EMB = 512
 TILES = SEQ // P
 EPS = 1e-5
-QUANT_AFTER = 6
+VECTOR_TILES = (0, 2)
+GPSIMD_TILE = 3
+GPSIMD_BIASES = 3
+QUANT_AFTER = 2
 
 FLOPS = 2 * N_B * SEQ * D_EMB * (2 * D_EMB)
 
@@ -62,6 +65,8 @@ def tile_causalfeaturetransformer_pa_t_kernel(
             raw = keep.tile([P, PACK, D_EMB], BF16, name="w_raw%d" % o)
             nc.sync.dma_start(out=raw[:], in_=weights[o].rearrange("(q t) e -> q t e", t=PACK))
             w_raw.append(raw)
+        shift_col = keep.tile([P, 1, PACK], BF16)
+        nc.sync.dma_start(out=shift_col[:, 0, :], in_=be1.rearrange("(q t) -> q t", t=PACK))
         bias_all = keep.tile([P, 2, D_EMB], BF16)
         for o in range(2):
             nc.sync.dma_start(out=bias_all[:, o, :], in_=biases[o].partition_broadcast(P))
@@ -159,6 +164,10 @@ def tile_causalfeaturetransformer_pa_t_kernel(
         w_grouped = [
             keep.tile([P, D_EMB, PACK], BF16, name="w_grouped%d" % o, align_bytes=64) for o in range(2)
         ]
+        half = D_EMB // 2
+        nc.scalar.copy(
+            out=w_grouped[1][:, half:D_EMB, :], in_=w_raw[1][:, :, half:D_EMB].rearrange("q t e -> q e t")
+        )
         nc.gpsimd.tensor_scalar(
             out=w_grouped[0][:],
             in0=w_raw[0][:].rearrange("q t e -> q e t"),
@@ -168,8 +177,8 @@ def tile_causalfeaturetransformer_pa_t_kernel(
             op1=ALU.add,
         )
         nc.gpsimd.tensor_scalar(
-            out=w_grouped[1][:],
-            in0=w_raw[1][:].rearrange("q t e -> q e t"),
+            out=w_grouped[1][:, 0:half, :],
+            in0=w_raw[1][:, :, 0:half].rearrange("q t e -> q e t"),
             scalar1=1.0,
             scalar2=0.0,
             op0=ALU.mult,
@@ -190,34 +199,47 @@ def tile_causalfeaturetransformer_pa_t_kernel(
         codes_of = {}
         res_of = {}
 
-        def scale(n, j, on_vector=False):
+        def scale(n, j, engine):
             if j == 0:
-                z_of[n] = work.tile([P, TILES, D_EMB], F32, name="z")
+                z_of[n] = work.tile([P, TILES, D_EMB], F32, name="z", bufs=3)
             dst = z_of[n][:, j, :]
             src = centred[:, j, :, :].rearrange("p t q -> p (t q)")
             c = c_scale[:, j, n : n + 1]
-            if on_vector:
+            if engine == "vector":
                 nc.vector.tensor_scalar(out=dst, in0=src, scalar1=c, scalar2=None, op0=ALU.mult)
+            elif engine == "gpsimd":
+                nc.gpsimd.tensor_scalar(
+                    out=dst, in0=src, scalar1=c, scalar2=0.0, op0=ALU.mult, op1=ALU.add
+                )
             else:
                 nc.scalar.activation(out=dst, in_=src, func=ACT.Identity, scale=c)
 
         def turn(n, j):
             if j == 0:
                 grouped_of[n] = work.tile([P, SEQ, PACK], BF16, name="grouped", align_bytes=64)
+            dst = grouped_of[n][:, j * P : (j + 1) * P, :]
+            on_vector = n > 0 and j in VECTOR_TILES
             xn_t = psum_t.tile([P, PACK, P], F32, tag="t")
             for t in range(PACK):
-                for src, first in ((z_of[n][:, j, t * P : (t + 1) * P], True), (shift[:, t, :], False)):
+                sources = [z_of[n][:, j, t * P : (t + 1) * P]]
+                if not on_vector:
+                    sources.append(shift[:, t, :])
+                for k, src in enumerate(sources):
                     nc.tensor.matmul(
                         out=xn_t[:, t, :],
                         lhsT=src,
                         rhs=ident_f32[:],
-                        start=first,
-                        stop=not first,
+                        start=(k == 0),
+                        stop=(k == len(sources) - 1),
                         is_transpose=True,
                     )
-            nc.scalar.copy(
-                out=grouped_of[n][:, j * P : (j + 1) * P, :], in_=xn_t[:].rearrange("q t i -> q i t")
-            )
+            turned = xn_t[:].rearrange("q t i -> q i t")
+            if on_vector:
+                nc.vector.tensor_tensor(
+                    out=dst, in0=turned, in1=shift_col[:].to_broadcast([P, P, PACK]), op=ALU.add
+                )
+            else:
+                nc.scalar.copy(out=dst, in_=turned)
 
         def quantise(n, j0, j1):
             if j0 == 0:
@@ -248,9 +270,12 @@ def tile_causalfeaturetransformer_pa_t_kernel(
                 start=True,
                 stop=True,
             )
-            nc.vector.tensor_tensor(
-                out=res_of[n][o][:, j, :], in0=acc[:], in1=bias_all[:, o, :], op=ALU.add
-            )
+            dst = res_of[n][o][:, j, :]
+            if o == 1 and j < GPSIMD_BIASES:
+                nc.scalar.copy(out=dst, in_=acc[:])
+                nc.gpsimd.tensor_tensor(out=dst, in0=dst, in1=bias_all[:, o, :], op=ALU.add)
+            else:
+                nc.vector.tensor_tensor(out=dst, in0=acc[:], in1=bias_all[:, o, :], op=ALU.add)
             if j % 2 == 1:
                 nc.sync.dma_start(
                     out=out_views[o][n][:, j - 1 : j + 1, :], in_=res_of[n][o][:, j - 1 : j + 1, :]
@@ -259,9 +284,9 @@ def tile_causalfeaturetransformer_pa_t_kernel(
         for j in range(TILES):
             if j > 0:
                 centre(j)
-            scale(0, j, on_vector=True)
+            scale(0, j, "vector")
             turn(0, j)
-            scale(1, j)
+            scale(1, j, "scalar")
         quantise_weight(0)
         quantise_weight(1)
         quantise(0, 0, 1)
@@ -275,7 +300,7 @@ def tile_causalfeaturetransformer_pa_t_kernel(
             if j < 2:
                 for i in (2 * j, 2 * j + 1):
                     turn(1, i)
-                    scale(2, i)
+                    scale(2, i, "scalar")
 
         for n in range(N_B):
             for j in range(TILES):
@@ -288,4 +313,4 @@ def tile_causalfeaturetransformer_pa_t_kernel(
                     for i in (j - 1, j):
                         turn(n + 2, i)
                         if n + 3 < N_B:
-                            scale(n + 3, i)
+                            scale(n + 3, i, "gpsimd" if i == GPSIMD_TILE else "scalar")

@@ -22,6 +22,7 @@ EPS = 1e-5
 VECTOR_TILES = (0, 2)
 GPSIMD_TILE = 3
 GPSIMD_BIASES = 3
+LAST_BIASES = 2
 QUANT_AFTER = 2
 
 FLOPS = 2 * N_B * SEQ * D_EMB * (2 * D_EMB)
@@ -56,17 +57,17 @@ def tile_causalfeaturetransformer_pa_t_kernel(
             out=tokens[127:128, 0:3, :], in_=feat_emb[508:511].rearrange("(p j) d -> p j d", p=1)
         )
         nc.sync.dma_start(out=tokens[127:128, 3:4, :], in_=label_token)
-        gain_rows = keep.tile([P, 2, D_EMB], BF16)
+        gain_rows = keep.tile([P, D_EMB], BF16)
         nc.vector.memset(gain_rows[:], 0.0)
-        for k, vec in enumerate((g1, be1)):
-            nc.sync.dma_start(out=gain_rows[0:1, k, :], in_=vec.rearrange("(o d) -> o d", o=1))
+        nc.sync.dma_start(out=gain_rows[0:1, :], in_=g1.rearrange("(o d) -> o d", o=1))
+        shift_cols = keep.tile([P, P], BF16)
+        nc.gpsimd.memset(shift_cols[:], 0.0)
+        nc.sync.dma_start(out=shift_cols[:, 0:PACK], in_=be1.rearrange("(q t) -> q t", t=PACK))
         w_raw = []
         for o in range(2):
             raw = keep.tile([P, PACK, D_EMB], BF16, name="w_raw%d" % o)
             nc.sync.dma_start(out=raw[:], in_=weights[o].rearrange("(q t) e -> q t e", t=PACK))
             w_raw.append(raw)
-        shift_col = keep.tile([P, 1, PACK], BF16)
-        nc.sync.dma_start(out=shift_col[:, 0, :], in_=be1.rearrange("(q t) -> q t", t=PACK))
         bias_all = keep.tile([P, 2, D_EMB], BF16)
         for o in range(2):
             nc.sync.dma_start(out=bias_all[:, o, :], in_=biases[o].partition_broadcast(P))
@@ -83,6 +84,8 @@ def tile_causalfeaturetransformer_pa_t_kernel(
         nc.vector.memset(ones[:], 1.0)
         ident_f32 = keep.tile([P, P], F32)
         make_identity(nc, ident_f32[:])
+        ident_bf16 = keep.tile([P, P], BF16)
+        make_identity(nc, ident_bf16[:])
         zn_rows = keep.tile([P, SEQ], F32)
         nc.vector.memset(zn_rows[:], 0.0)
         nc.vector.memset(zn_rows[0:N_B, SEQ - 1 : SEQ], 1.0)
@@ -115,22 +118,30 @@ def tile_causalfeaturetransformer_pa_t_kernel(
         for j in range(TILES):
             nc.tensor.transpose(zn_psum[:, j, :], zn_rows[:, j * P : (j + 1) * P], ident_f32[:])
 
-        spread = []
-        for k in range(2):
-            row_psum = psum_t.tile([P, D_EMB], F32, tag="t")
-            nc.tensor.matmul(
-                out=row_psum[:], lhsT=ones[:], rhs=gain_rows[:, k, :], start=True, stop=True
-            )
-            row = keep.tile([P, PACK, P], F32, name="spread%d" % k)
-            nc.scalar.copy(out=row[:], in_=row_psum[:].rearrange("p (q t) -> p t q", t=PACK))
-            spread.append(row)
-        gain, shift = spread
+        gain_psum = psum_t.tile([P, D_EMB], F32, tag="t")
+        nc.tensor.matmul(out=gain_psum[:], lhsT=ones[:], rhs=gain_rows[:], start=True, stop=True)
+        gain = keep.tile([P, PACK, P], F32)
+        nc.scalar.copy(out=gain[:], in_=gain_psum[:].rearrange("p (q t) -> p t q", t=PACK))
+        shift_psum = psum_t.tile([P, P], BF16, tag="t")
+        nc.tensor.transpose(shift_psum[:], shift_cols[:], ident_bf16[:])
+        shift_rows = keep.tile([P, P], BF16)
+        nc.scalar.copy(out=shift_rows[:], in_=shift_psum[:])
+        picks = keep.tile([P, PACK, P], BF16)
+        nc.scalar.copy(
+            out=picks[:], in_=ident_bf16[:, 0:PACK].unsqueeze(2).to_broadcast([P, PACK, P])
+        )
 
         tok_stats = keep.tile([P, TILES, 6], F32)
         tok_mv = keep.tile([P, TILES, 2], F32)
+        shape_c = [P, TILES, N_B]
+        zn_cols = keep.tile(shape_c, F32)
+        zn_sq = keep.tile(shape_c, F32)
         for j in range(TILES):
             nc.vector.bn_stats(out=tok_stats[:, j, :], in_=tokens[:, j, :])
             nc.vector.bn_aggr(out=tok_mv[:, j, :], in_=tok_stats[:, j, :])
+            if j == 1:
+                nc.vector.tensor_copy(out=zn_cols[:], in_=zn_psum[:, :, 0:N_B])
+                nc.vector.tensor_tensor(out=zn_sq[:], in0=zn_cols[:], in1=zn_cols[:], op=ALU.mult)
 
         centred = keep.tile([P, TILES, PACK, P], F32)
 
@@ -144,11 +155,6 @@ def tile_causalfeaturetransformer_pa_t_kernel(
                 op1=ALU.mult,
             )
 
-        shape_c = [P, TILES, N_B]
-        zn_cols = keep.tile(shape_c, F32)
-        nc.vector.tensor_copy(out=zn_cols[:], in_=zn_psum[:, :, 0:N_B])
-        zn_sq = keep.tile(shape_c, F32)
-        nc.vector.tensor_tensor(out=zn_sq[:], in0=zn_cols[:], in1=zn_cols[:], op=ALU.mult)
         x_var = keep.tile(shape_c, F32)
         nc.vector.tensor_tensor(
             out=x_var[:], in0=zn_sq[:], in1=tok_mv[:, :, 1:2].to_broadcast(shape_c), op=ALU.mult
@@ -199,6 +205,9 @@ def tile_causalfeaturetransformer_pa_t_kernel(
         codes_of = {}
         res_of = {}
 
+        def scaler(j):
+            return "gpsimd" if j == GPSIMD_TILE else "scalar"
+
         def scale(n, j, engine):
             if j == 0:
                 z_of[n] = work.tile([P, TILES, D_EMB], F32, name="z", bufs=3)
@@ -221,24 +230,26 @@ def tile_causalfeaturetransformer_pa_t_kernel(
             on_vector = n > 0 and j in VECTOR_TILES
             xn_t = psum_t.tile([P, PACK, P], F32, tag="t")
             for t in range(PACK):
-                sources = [z_of[n][:, j, t * P : (t + 1) * P]]
-                if not on_vector:
-                    sources.append(shift[:, t, :])
-                for k, src in enumerate(sources):
-                    nc.tensor.matmul(
-                        out=xn_t[:, t, :],
-                        lhsT=src,
-                        rhs=ident_f32[:],
-                        start=(k == 0),
-                        stop=(k == len(sources) - 1),
-                        is_transpose=True,
-                    )
+                nc.tensor.matmul(
+                    out=xn_t[:, t, :],
+                    lhsT=z_of[n][:, j, t * P : (t + 1) * P],
+                    rhs=ident_f32[:],
+                    start=(t == 0),
+                    stop=(on_vector and t == PACK - 1),
+                    is_transpose=True,
+                )
             turned = xn_t[:].rearrange("q t i -> q i t")
             if on_vector:
-                nc.vector.tensor_tensor(
-                    out=dst, in0=turned, in1=shift_col[:].to_broadcast([P, P, PACK]), op=ALU.add
-                )
+                shift = shift_cols[:, 0:PACK].unsqueeze(1).to_broadcast([P, P, PACK])
+                nc.vector.tensor_tensor(out=dst, in0=turned, in1=shift, op=ALU.add)
             else:
+                nc.tensor.matmul(
+                    out=xn_t[:].rearrange("q t i -> q (t i)"),
+                    lhsT=shift_rows[:],
+                    rhs=picks[:].rearrange("k t i -> k (t i)"),
+                    start=False,
+                    stop=True,
+                )
                 nc.scalar.copy(out=dst, in_=turned)
 
         def quantise(n, j0, j1):
@@ -271,7 +282,7 @@ def tile_causalfeaturetransformer_pa_t_kernel(
                 stop=True,
             )
             dst = res_of[n][o][:, j, :]
-            if o == 1 and j < GPSIMD_BIASES:
+            if o == 1 and j < (GPSIMD_BIASES if n < N_B - 2 else LAST_BIASES):
                 nc.scalar.copy(out=dst, in_=acc[:])
                 nc.gpsimd.tensor_tensor(out=dst, in0=dst, in1=bias_all[:, o, :], op=ALU.add)
             else:
@@ -286,7 +297,7 @@ def tile_causalfeaturetransformer_pa_t_kernel(
                 centre(j)
             scale(0, j, "vector")
             turn(0, j)
-            scale(1, j, "scalar")
+            scale(1, j, scaler(j))
         quantise_weight(0)
         quantise_weight(1)
         quantise(0, 0, 1)
@@ -294,13 +305,15 @@ def tile_causalfeaturetransformer_pa_t_kernel(
             if j + 1 < TILES:
                 quantise(0, j + 1, j + 2)
             else:
-                quantise(1, 0, TILES)
+                quantise(1, 0, 2)
             for o in range(2):
                 project(0, j, o)
             if j < 2:
                 for i in (2 * j, 2 * j + 1):
                     turn(1, i)
-                    scale(2, i, "scalar")
+                    scale(2, i, scaler(i))
+
+        quantise(1, 2, TILES)
 
         for n in range(N_B):
             for j in range(TILES):
@@ -313,4 +326,4 @@ def tile_causalfeaturetransformer_pa_t_kernel(
                     for i in (j - 1, j):
                         turn(n + 2, i)
                         if n + 3 < N_B:
-                            scale(n + 3, i, "gpsimd" if i == GPSIMD_TILE else "scalar")
+                            scale(n + 3, i, scaler(i))

@@ -13,6 +13,7 @@ ACT = mybir.ActivationFunctionType
 
 P = 128
 PACK = 4
+RUN = 4
 N_B = 16
 D_FEAT = 511
 SEQ = 512
@@ -226,7 +227,6 @@ def tile_causalfeaturetransformer_pa_t_kernel(
         def turn(n, j):
             if j == 0:
                 grouped_of[n] = work.tile([P, SEQ, PACK], BF16, name="grouped", align_bytes=64)
-            dst = grouped_of[n][:, j * P : (j + 1) * P, :]
             on_vector = n > 0 and j in VECTOR_TILES
             xn_t = psum_t.tile([P, PACK, P], F32, tag="t")
             for t in range(PACK):
@@ -238,10 +238,13 @@ def tile_causalfeaturetransformer_pa_t_kernel(
                     stop=(on_vector and t == PACK - 1),
                     is_transpose=True,
                 )
-            turned = xn_t[:].rearrange("q t i -> q i t")
+            turned = xn_t[:].rearrange("q t (c i) -> q c t i", i=RUN)
+            dst = grouped_of[n][:, j * P : (j + 1) * P, :].rearrange("q (c i) t -> q c t i", i=RUN)
             if on_vector:
-                shift = shift_cols[:, 0:PACK].unsqueeze(1).to_broadcast([P, P, PACK])
-                nc.vector.tensor_tensor(out=dst, in0=turned, in1=shift, op=ALU.add)
+                shift = shift_cols[:, 0:PACK].unsqueeze(1).unsqueeze(3)
+                nc.vector.tensor_tensor(
+                    out=dst, in0=turned, in1=shift.to_broadcast([P, P // RUN, PACK, RUN]), op=ALU.add
+                )
             else:
                 nc.tensor.matmul(
                     out=xn_t[:].rearrange("q t i -> q (t i)"),

@@ -21,9 +21,9 @@ D_EMB = 512
 TILES = SEQ // P
 EPS = 1e-5
 VECTOR_TILES = (0, 2)
+GPSIMD_BIASES = (0, 2)
+ODD_ROW_BIASES = (0, 1, 2)
 GPSIMD_TILE = 3
-GPSIMD_BIASES = 3
-LAST_BIASES = 2
 QUANT_AFTER = 2
 
 FLOPS = 2 * N_B * SEQ * D_EMB * (2 * D_EMB)
@@ -285,7 +285,7 @@ def tile_causalfeaturetransformer_pa_t_kernel(
                 stop=True,
             )
             dst = res_of[n][o][:, j, :]
-            if o == 1 and j < (GPSIMD_BIASES if n < N_B - 2 else LAST_BIASES):
+            if o == 1 and j in (ODD_ROW_BIASES if n % 2 == 1 and n < N_B - 2 else GPSIMD_BIASES):
                 nc.scalar.copy(out=dst, in_=acc[:])
                 nc.gpsimd.tensor_tensor(out=dst, in0=dst, in1=bias_all[:, o, :], op=ALU.add)
             else:

@@ -20,11 +20,9 @@ SEQ = 512
 D_EMB = 512
 TILES = SEQ // P
 EPS = 1e-5
-VECTOR_TILES = (0, 2)
-GPSIMD_BIASES = (0, 2)
-ODD_ROW_BIASES = (0, 1, 2)
-GPSIMD_TILE = 3
-QUANT_AFTER = 2
+WORD_TILES = 2
+GPSIMD_BIASES = (0, 1, 3)
+LAST_ROW_BIASES = (0, 1)
 
 FLOPS = 2 * N_B * SEQ * D_EMB * (2 * D_EMB)
 
@@ -42,33 +40,35 @@ def tile_causalfeaturetransformer_pa_t_kernel(
         keep = ctx.enter_context(tc.tile_pool(name="keep", bufs=1))
         work = ctx.enter_context(tc.tile_pool(name="work", bufs=2))
         results = ctx.enter_context(tc.tile_pool(name="results", bufs=3))
-        psum_t = ctx.enter_context(tc.psum_pool(name="psum_t", bufs=4))
+        psum_keep = ctx.enter_context(tc.psum_pool(name="psum_keep", bufs=1))
+        psum_t = ctx.enter_context(tc.psum_pool(name="psum_t", bufs=3))
         psum_mx = ctx.enter_context(tc.psum_pool(name="psum_mx", bufs=4))
 
         z_raw = keep.tile([N_B, D_FEAT], BF16)
         nc.sync.dma_start(out=z_raw[:], in_=Z)
         tokens = keep.tile([P, TILES, D_EMB], BF16)
-        nc.sync.dma_start(
-            out=tokens[0:112], in_=feat_emb[0:448].rearrange("(p j) d -> p j d", j=TILES)
-        )
-        nc.sync.dma_start(
-            out=tokens[112:127], in_=feat_emb[448:508].rearrange("(p j) d -> p j d", j=TILES)
-        )
-        nc.sync.dma_start(
-            out=tokens[127:128, 0:3, :], in_=feat_emb[508:511].rearrange("(p j) d -> p j d", p=1)
-        )
-        nc.sync.dma_start(out=tokens[127:128, 3:4, :], in_=label_token)
-        gain_rows = keep.tile([P, D_EMB], BF16)
-        nc.vector.memset(gain_rows[:], 0.0)
-        nc.sync.dma_start(out=gain_rows[0:1, :], in_=g1.rearrange("(o d) -> o d", o=1))
+
+        def load_tokens(j, p0, p1):
+            nc.sync.dma_start(
+                out=tokens[p0:p1, j, :], in_=feat_emb[p0 * TILES + j : (p1 - 1) * TILES + j + 1 : TILES]
+            )
+
+        rows = keep.tile([P, 2, D_EMB], BF16)
+        nc.vector.memset(rows[:], 0.0)
+        load_tokens(0, 0, P)
+        load_tokens(1, 0, P)
+        nc.scalar.dma_start(out=rows[0:1, 0, :], in_=g1.rearrange("(o d) -> o d", o=1))
+        load_tokens(2, 0, P)
+        load_tokens(3, 0, P // 2)
+        w_raw = [keep.tile([P, PACK, D_EMB], BF16, name="w_raw%d" % o) for o in range(2)]
+        nc.sync.dma_start(out=w_raw[0][:], in_=weights[0].rearrange("(q t) e -> q t e", t=PACK))
+        nc.scalar.dma_start(out=rows[0:1, 1, :], in_=be1.rearrange("(o d) -> o d", o=1))
+        load_tokens(3, P // 2, P - 1)
+        nc.sync.dma_start(out=tokens[P - 1 : P, 3:4, :], in_=label_token)
+        nc.sync.dma_start(out=w_raw[1][:], in_=weights[1].rearrange("(q t) e -> q t e", t=PACK))
         shift_cols = keep.tile([P, P], BF16)
-        nc.gpsimd.memset(shift_cols[:], 0.0)
+        nc.vector.memset(shift_cols[:], 0.0)
         nc.sync.dma_start(out=shift_cols[:, 0:PACK], in_=be1.rearrange("(q t) -> q t", t=PACK))
-        w_raw = []
-        for o in range(2):
-            raw = keep.tile([P, PACK, D_EMB], BF16, name="w_raw%d" % o)
-            nc.sync.dma_start(out=raw[:], in_=weights[o].rearrange("(q t) e -> q t e", t=PACK))
-            w_raw.append(raw)
         bias_all = keep.tile([P, 2, D_EMB], BF16)
         for o in range(2):
             nc.sync.dma_start(out=bias_all[:, o, :], in_=biases[o].partition_broadcast(P))
@@ -76,7 +76,7 @@ def tile_causalfeaturetransformer_pa_t_kernel(
         one_col = keep.tile([P, 1], F32)
         nc.vector.memset(one_col[:], 1.0)
         warm = keep.tile([P, 1], F32)
-        nc.scalar.activation(out=warm[:], in_=one_col[:], func=ACT.Sqrt)
+        nc.scalar.activation(out=warm[:], in_=one_col[:], func=ACT.Abs_reciprocal_sqrt)
         eps_col = keep.tile([P, 1], F32)
         nc.vector.tensor_scalar(
             out=eps_col[:], in0=one_col[:], scalar1=0.0, scalar2=EPS, op0=ALU.mult, op1=ALU.add
@@ -91,16 +91,30 @@ def tile_causalfeaturetransformer_pa_t_kernel(
         nc.vector.memset(zn_rows[:], 0.0)
         nc.vector.memset(zn_rows[0:N_B, SEQ - 1 : SEQ], 1.0)
 
+        gain = psum_mx.tile([P, D_EMB], F32, name="acc")
+        nc.tensor.matmul(out=gain[:], lhsT=ones[:], rhs=rows[:, 0, :], start=True, stop=True)
+        shift_w = psum_keep.tile([P, 2, 2 * P], F32)
+        for u in range(2):
+            nc.tensor.matmul(
+                out=shift_w[:, u, :],
+                lhsT=ones[:],
+                rhs=rows[:, 1, :].rearrange("k (q u e) -> k u q e", u=2, e=2)[:, u, :, :],
+                start=True,
+                stop=True,
+            )
+
+        tok_stats = keep.tile([P, TILES, 6], F32)
+        tok_mv = keep.tile([P, TILES, 2], F32)
         z_stats = keep.tile([N_B, 6], F32)
         nc.vector.bn_stats(out=z_stats[:], in_=z_raw[:])
+        nc.vector.bn_stats(out=tok_stats[:, 0, :], in_=tokens[:, 0, :])
         z_mv = keep.tile([N_B, 2], F32)
         nc.vector.bn_aggr(out=z_mv[:], in_=z_stats[:])
-        z_sd = keep.tile([N_B, 1], F32)
-        nc.scalar.activation(
-            out=z_sd[:], in_=z_mv[:, 1:2], func=ACT.Sqrt, bias=eps_col[0:N_B, :]
-        )
         z_rstd = keep.tile([N_B, 1], F32)
-        nc.vector.reciprocal(out=z_rstd[:], in_=z_sd[:])
+        nc.scalar.activation(
+            out=z_rstd[:], in_=z_mv[:, 1:2], func=ACT.Abs_reciprocal_sqrt, bias=eps_col[0:N_B, :]
+        )
+        nc.vector.bn_stats(out=tok_stats[:, 1, :], in_=tokens[:, 1, :])
         zn_view = zn_rows[0:N_B, :].rearrange("n (j p) -> n j p", j=TILES)
         full = (P - 1) * TILES
         for dst, cols in (
@@ -115,84 +129,73 @@ def tile_causalfeaturetransformer_pa_t_kernel(
                 op0=ALU.subtract,
                 op1=ALU.mult,
             )
+        for j in range(2):
+            nc.vector.bn_aggr(out=tok_mv[:, j, :], in_=tok_stats[:, j, :])
         zn_psum = psum_t.tile([P, TILES, P], F32, tag="t")
         for j in range(TILES):
             nc.tensor.transpose(zn_psum[:, j, :], zn_rows[:, j * P : (j + 1) * P], ident_f32[:])
 
-        gain_psum = psum_t.tile([P, D_EMB], F32, tag="t")
-        nc.tensor.matmul(out=gain_psum[:], lhsT=ones[:], rhs=gain_rows[:], start=True, stop=True)
-        gain = keep.tile([P, PACK, P], F32)
-        nc.scalar.copy(out=gain[:], in_=gain_psum[:].rearrange("p (q t) -> p t q", t=PACK))
-        shift_psum = psum_t.tile([P, P], BF16, tag="t")
-        nc.tensor.transpose(shift_psum[:], shift_cols[:], ident_bf16[:])
-        shift_rows = keep.tile([P, P], BF16)
-        nc.scalar.copy(out=shift_rows[:], in_=shift_psum[:])
-        picks = keep.tile([P, PACK, P], BF16)
-        nc.scalar.copy(
-            out=picks[:], in_=ident_bf16[:, 0:PACK].unsqueeze(2).to_broadcast([P, PACK, P])
-        )
-
-        tok_stats = keep.tile([P, TILES, 6], F32)
-        tok_mv = keep.tile([P, TILES, 2], F32)
-        shape_c = [P, TILES, N_B]
-        zn_cols = keep.tile(shape_c, F32)
-        zn_sq = keep.tile(shape_c, F32)
-        for j in range(TILES):
-            nc.vector.bn_stats(out=tok_stats[:, j, :], in_=tokens[:, j, :])
-            nc.vector.bn_aggr(out=tok_mv[:, j, :], in_=tok_stats[:, j, :])
-            if j == 1:
-                nc.vector.tensor_copy(out=zn_cols[:], in_=zn_psum[:, :, 0:N_B])
-                nc.vector.tensor_tensor(out=zn_sq[:], in0=zn_cols[:], in1=zn_cols[:], op=ALU.mult)
-
-        centred = keep.tile([P, TILES, PACK, P], F32)
+        centred_w = keep.tile([P, WORD_TILES, 2, P, 2], F32)
+        centred = keep.tile([P, TILES - WORD_TILES, PACK, P], F32)
 
         def centre(j):
-            nc.vector.scalar_tensor_tensor(
-                out=centred[:, j, :, :],
-                in0=tokens[:, j, :].rearrange("p (q t) -> p t q", t=PACK),
-                scalar=tok_mv[:, j, 0:1],
-                in1=gain[:],
-                op0=ALU.subtract,
-                op1=ALU.mult,
+            if j < WORD_TILES:
+                parts = [
+                    (centred_w[:, j, u, :, :], "p (q u e) -> p u q e", {"u": 2, "e": 2}, u) for u in range(2)
+                ]
+            else:
+                parts = [(centred[:, j - WORD_TILES, :, :], "p (o q t) -> p o t q", {"o": 1, "t": PACK}, 0)]
+            for dst, order, sizes, i in parts:
+                nc.vector.scalar_tensor_tensor(
+                    out=dst,
+                    in0=tokens[:, j, :].rearrange(order, **sizes)[:, i, :, :],
+                    scalar=tok_mv[:, j, 0:1],
+                    in1=gain[:].rearrange(order, **sizes)[:, i, :, :],
+                    op0=ALU.subtract,
+                    op1=ALU.mult,
+                )
+
+        shape_c = [P, TILES, N_B]
+        zn_sq = keep.tile(shape_c, F32)
+        x_rstd = keep.tile(shape_c, F32)
+        c_scale = keep.tile(shape_c, F32)
+
+        def scales_of_tiles(j0, j1):
+            for j in range(j0, j1):
+                nc.scalar.activation(
+                    out=x_rstd[:, j, :],
+                    in_=zn_sq[:, j, :],
+                    func=ACT.Abs_reciprocal_sqrt,
+                    scale=tok_mv[:, j, 1:2],
+                    bias=eps_col[:],
+                )
+            nc.vector.tensor_tensor(
+                out=c_scale[:, j0:j1, :], in0=zn_psum[:, j0:j1, 0:N_B], in1=x_rstd[:, j0:j1, :], op=ALU.mult
             )
 
-        x_var = keep.tile(shape_c, F32)
-        nc.vector.tensor_tensor(
-            out=x_var[:], in0=zn_sq[:], in1=tok_mv[:, :, 1:2].to_broadcast(shape_c), op=ALU.mult
-        )
-        x_sd = keep.tile(shape_c, F32)
-        nc.scalar.activation(out=x_sd[:], in_=x_var[:], func=ACT.Sqrt, bias=eps_col[:])
+        nc.vector.bn_stats(out=tok_stats[:, 2, :], in_=tokens[:, 2, :])
         centre(0)
-        x_rstd = keep.tile(shape_c, F32)
-        nc.vector.reciprocal(out=x_rstd[:], in_=x_sd[:])
-        c_scale = keep.tile(shape_c, F32)
-        nc.vector.tensor_tensor(out=c_scale[:], in0=zn_cols[:], in1=x_rstd[:], op=ALU.mult)
+        nc.scalar.activation(out=zn_sq[:], in_=zn_psum[:, :, 0:N_B], func=ACT.Square)
+        centre(1)
+        nc.vector.bn_aggr(out=tok_mv[:, 2, :], in_=tok_stats[:, 2, :])
+        scales_of_tiles(0, 2)
+        nc.vector.bn_stats(out=tok_stats[:, 3, :], in_=tokens[:, 3, :])
 
         w_grouped = [
             keep.tile([P, D_EMB, PACK], BF16, name="w_grouped%d" % o, align_bytes=64) for o in range(2)
         ]
-        half = D_EMB // 2
-        nc.scalar.copy(
-            out=w_grouped[1][:, half:D_EMB, :], in_=w_raw[1][:, :, half:D_EMB].rearrange("q t e -> q e t")
-        )
-        nc.gpsimd.tensor_scalar(
-            out=w_grouped[0][:],
-            in0=w_raw[0][:].rearrange("q t e -> q e t"),
-            scalar1=1.0,
-            scalar2=0.0,
-            op0=ALU.mult,
-            op1=ALU.add,
-        )
-        nc.gpsimd.tensor_scalar(
-            out=w_grouped[1][:, 0:half, :],
-            in0=w_raw[1][:, :, 0:half].rearrange("q t e -> q e t"),
-            scalar1=1.0,
-            scalar2=0.0,
-            op0=ALU.mult,
-            op1=ALU.add,
-        )
         w_codes = [keep.tile([P, D_EMB], U32, name="w_codes%d" % o, align_bytes=64) for o in range(2)]
         w_scales = [keep.tile([P, D_EMB], U8, name="w_scales%d" % o, align_bytes=64) for o in range(2)]
+
+        def regroup(o, e0, e1, engine):
+            dst = w_grouped[o][:, e0:e1, :]
+            src = w_raw[o][:, :, e0:e1].rearrange("q t e -> q e t")
+            if engine == "scalar":
+                nc.scalar.copy(out=dst, in_=src)
+            elif engine == "vector":
+                nc.vector.tensor_copy(out=dst, in_=src)
+            else:
+                nc.gpsimd.tensor_scalar(out=dst, in0=src, scalar1=1.0, scalar2=0.0, op0=ALU.mult, op1=ALU.add)
 
         def quantise_weight(o):
             nc.vector.quantize_mx(
@@ -201,59 +204,91 @@ def tile_causalfeaturetransformer_pa_t_kernel(
                 in_=w_grouped[o][:].rearrange("q e t -> q (e t)"),
             )
 
+        shift_rows = keep.tile([P, P], BF16)
+        picks = keep.tile([P, PACK, P], BF16)
+        nc.scalar.copy(
+            out=picks[:], in_=ident_bf16[:, 0:PACK].unsqueeze(2).to_broadcast([P, PACK, P])
+        )
+
+        def shift_product_operands():
+            shift_psum = psum_t.tile([P, P], BF16, tag="t")
+            nc.tensor.transpose(shift_psum[:], shift_cols[:], ident_bf16[:])
+            nc.scalar.copy(out=shift_rows[:], in_=shift_psum[:])
+
         z_of = {}
+        words_of = {}
         grouped_of = {}
         codes_of = {}
         res_of = {}
 
-        def scaler(j):
-            return "gpsimd" if j == GPSIMD_TILE else "scalar"
+        def finish(n, j):
+            if j == 0:
+                words_of[n] = work.tile([P, WORD_TILES, D_EMB], BF16, name="words", align_bytes=64, bufs=6)
+            nc.vector.scalar_tensor_tensor(
+                out=words_of[n][:, j, :],
+                in0=centred_w[:, j, :, :, :].rearrange("p u q e -> p (u q e)"),
+                scalar=c_scale[:, j, n : n + 1],
+                in1=shift_w[:].rearrange("p u w -> p (u w)"),
+                op0=ALU.mult,
+                op1=ALU.add,
+            )
 
         def scale(n, j, engine):
-            if j == 0:
-                z_of[n] = work.tile([P, TILES, D_EMB], F32, name="z", bufs=3)
-            dst = z_of[n][:, j, :]
-            src = centred[:, j, :, :].rearrange("p t q -> p (t q)")
+            if j == WORD_TILES:
+                z_of[n] = work.tile([P, TILES - WORD_TILES, D_EMB], F32, name="z", bufs=3)
+            dst = z_of[n][:, j - WORD_TILES, :]
+            src = centred[:, j - WORD_TILES, :, :].rearrange("p t q -> p (t q)")
             c = c_scale[:, j, n : n + 1]
-            if engine == "vector":
-                nc.vector.tensor_scalar(out=dst, in0=src, scalar1=c, scalar2=None, op0=ALU.mult)
-            elif engine == "gpsimd":
+            if engine == "gpsimd":
                 nc.gpsimd.tensor_scalar(
                     out=dst, in0=src, scalar1=c, scalar2=0.0, op0=ALU.mult, op1=ALU.add
                 )
             else:
                 nc.scalar.activation(out=dst, in_=src, func=ACT.Identity, scale=c)
 
-        def turn(n, j):
-            if j == 0:
+        def turn_words(n, j0, j1):
+            if j0 == 0:
                 grouped_of[n] = work.tile([P, SEQ, PACK], BF16, name="grouped", align_bytes=64)
-            on_vector = n > 0 and j in VECTOR_TILES
-            xn_t = psum_t.tile([P, PACK, P], F32, tag="t")
-            for t in range(PACK):
+            words_t = psum_t.tile([P, WORD_TILES, 2, P], F32, tag="t")
+            for j in range(j0, j1):
+                words = words_of[n][:, j, :].bitcast(F32)
+                for u in range(2):
+                    nc.tensor.transpose(words_t[:, j - j0, u, :], words[:, u * P : (u + 1) * P], ident_f32[:])
+            nc.scalar.copy(
+                out=grouped_of[n][:, j0 * P : j1 * P, :]
+                .rearrange("q i t -> q (i t)")
+                .bitcast(F32)
+                .rearrange("q (j i u) -> q j i u", j=j1 - j0, u=2),
+                in_=words_t[:, 0 : j1 - j0, :, :].rearrange("q j u i -> q j i u"),
+            )
+
+        def turn(n, tiles):
+            turned = {}
+            for j in tiles:
+                xn_t = psum_t.tile([P, PACK, P], F32, tag="t")
+                turned[j] = xn_t
+                for t in range(PACK):
+                    nc.tensor.matmul(
+                        out=xn_t[:, t, :],
+                        lhsT=z_of[n][:, j - WORD_TILES, t * P : (t + 1) * P],
+                        rhs=ident_f32[:],
+                        start=(t == 0),
+                        stop=False,
+                        is_transpose=True,
+                    )
+            for j in tiles:
                 nc.tensor.matmul(
-                    out=xn_t[:, t, :],
-                    lhsT=z_of[n][:, j, t * P : (t + 1) * P],
-                    rhs=ident_f32[:],
-                    start=(t == 0),
-                    stop=(on_vector and t == PACK - 1),
-                    is_transpose=True,
-                )
-            turned = xn_t[:].rearrange("q t (c i) -> q c t i", i=RUN)
-            dst = grouped_of[n][:, j * P : (j + 1) * P, :].rearrange("q (c i) t -> q c t i", i=RUN)
-            if on_vector:
-                shift = shift_cols[:, 0:PACK].unsqueeze(1).unsqueeze(3)
-                nc.vector.tensor_tensor(
-                    out=dst, in0=turned, in1=shift.to_broadcast([P, P // RUN, PACK, RUN]), op=ALU.add
-                )
-            else:
-                nc.tensor.matmul(
-                    out=xn_t[:].rearrange("q t i -> q (t i)"),
+                    out=turned[j][:].rearrange("q t i -> q (t i)"),
                     lhsT=shift_rows[:],
                     rhs=picks[:].rearrange("k t i -> k (t i)"),
                     start=False,
                     stop=True,
                 )
-                nc.scalar.copy(out=dst, in_=turned)
+            for j in tiles:
+                nc.scalar.copy(
+                    out=grouped_of[n][:, j * P : (j + 1) * P, :].rearrange("q (c i) t -> q c t i", i=RUN),
+                    in_=turned[j][:].rearrange("q t (c i) -> q c t i", i=RUN),
+                )
 
         def quantise(n, j0, j1):
             if j0 == 0:
@@ -285,7 +320,7 @@ def tile_causalfeaturetransformer_pa_t_kernel(
                 stop=True,
             )
             dst = res_of[n][o][:, j, :]
-            if o == 1 and j in (ODD_ROW_BIASES if n % 2 == 1 and n < N_B - 2 else GPSIMD_BIASES):
+            if 2 * j + o in (LAST_ROW_BIASES if n == N_B - 1 else GPSIMD_BIASES):
                 nc.scalar.copy(out=dst, in_=acc[:])
                 nc.gpsimd.tensor_tensor(out=dst, in0=dst, in1=bias_all[:, o, :], op=ALU.add)
             else:
@@ -295,38 +330,78 @@ def tile_causalfeaturetransformer_pa_t_kernel(
                     out=out_views[o][n][:, j - 1 : j + 1, :], in_=res_of[n][o][:, j - 1 : j + 1, :]
                 )
 
-        for j in range(TILES):
-            if j > 0:
-                centre(j)
-            scale(0, j, "vector")
-            turn(0, j)
-            scale(1, j, scaler(j))
-        quantise_weight(0)
-        quantise_weight(1)
-        quantise(0, 0, 1)
-        for j in range(TILES):
-            if j + 1 < TILES:
-                quantise(0, j + 1, j + 2)
-            else:
-                quantise(1, 0, 2)
+        def project_pair(n, j):
             for o in range(2):
-                project(0, j, o)
-            if j < 2:
-                for i in (2 * j, 2 * j + 1):
-                    turn(1, i)
-                    scale(2, i, scaler(i))
+                project(n, j, o)
 
-        quantise(1, 2, TILES)
+        def scale_rest(n):
+            for j in range(WORD_TILES, TILES):
+                scale(n, j, "scalar")
 
-        for n in range(N_B):
-            for j in range(TILES):
-                if n > 0:
-                    for o in range(2):
-                        if 2 * j + o == QUANT_AFTER and n + 1 < N_B:
-                            quantise(n + 1, 0, TILES)
-                        project(n, j, o)
-                if j % 2 == 1 and n + 2 < N_B:
-                    for i in (j - 1, j):
-                        turn(n + 2, i)
-                        if n + 3 < N_B:
-                            scale(n + 3, i, scaler(i))
+        def turn_row(n):
+            turn_words(n, 0, WORD_TILES)
+            turn(n, range(WORD_TILES, TILES))
+
+        half = D_EMB // 2
+        regroup(0, 0, half, "gpsimd")
+        regroup(0, half, D_EMB, "gpsimd")
+        regroup(1, 0, half, "gpsimd")
+        regroup(1, half, D_EMB, "scalar")
+        finish(0, 0)
+        turn_words(0, 0, 1)
+        nc.vector.bn_aggr(out=tok_mv[:, 3, :], in_=tok_stats[:, 3, :])
+        finish(0, 1)
+        turn_words(0, 1, 2)
+        scales_of_tiles(2, TILES)
+        shift_product_operands()
+        quantise_weight(0)
+        quantise(0, 0, 1)
+        project(0, 0, 0)
+        centre(2)
+        scale(0, 2, "scalar")
+        quantise_weight(1)
+        centre(3)
+        scale(0, 3, "gpsimd")
+        turn(0, (2,))
+        project(0, 0, 1)
+        quantise(0, 1, 2)
+        finish(1, 0)
+        finish(1, 1)
+        project_pair(0, 1)
+        turn(0, (3,))
+        turn_words(1, 0, WORD_TILES)
+        scale_rest(1)
+        quantise(0, 2, 4)
+        project_pair(0, 2)
+        turn(1, (2, 3))
+        scale_rest(2)
+        finish(2, 0)
+        project_pair(0, 3)
+        finish(2, 1)
+        quantise(1, 0, TILES)
+        turn_row(2)
+        scale_rest(3)
+        finish(3, 0)
+        finish(3, 1)
+
+        for n in range(1, N_B):
+            if 1 < n < N_B - 1:
+                quantise(n + 1, 0, TILES)
+            project_pair(n, 0)
+            project_pair(n, 1)
+            if n == 1:
+                quantise(2, 0, TILES)
+            if n + 3 < N_B:
+                finish(n + 3, 0)
+                finish(n + 3, 1)
+            if n + 2 < N_B:
+                turn_words(n + 2, 0, WORD_TILES)
+                turn(n + 2, (2,))
+            project_pair(n, 2)
+            if n + 2 < N_B:
+                if n + 3 < N_B:
+                    scale(n + 3, 2, "scalar")
+                turn(n + 2, (3,))
+            project_pair(n, 3)
+            if n + 3 < N_B:
+                scale(n + 3, 3, "scalar")

@@ -41,8 +41,8 @@ def tile_causalfeaturetransformer_pa_t_kernel(
         work = ctx.enter_context(tc.tile_pool(name="work", bufs=2))
         results = ctx.enter_context(tc.tile_pool(name="results", bufs=3))
         psum_keep = ctx.enter_context(tc.psum_pool(name="psum_keep", bufs=1))
-        psum_t = ctx.enter_context(tc.psum_pool(name="psum_t", bufs=3))
-        psum_mx = ctx.enter_context(tc.psum_pool(name="psum_mx", bufs=4))
+        psum_t = ctx.enter_context(tc.psum_pool(name="psum_t", bufs=2))
+        psum_mx = ctx.enter_context(tc.psum_pool(name="psum_mx", bufs=5))
 
         z_raw = keep.tile([N_B, D_FEAT], BF16)
         nc.sync.dma_start(out=z_raw[:], in_=Z)
@@ -160,7 +160,7 @@ def tile_causalfeaturetransformer_pa_t_kernel(
         x_rstd = keep.tile(shape_c, F32)
         c_scale = keep.tile(shape_c, F32)
 
-        def scales_of_tiles(j0, j1):
+        def spreads(j0, j1):
             for j in range(j0, j1):
                 nc.scalar.activation(
                     out=x_rstd[:, j, :],
@@ -169,6 +169,8 @@ def tile_causalfeaturetransformer_pa_t_kernel(
                     scale=tok_mv[:, j, 1:2],
                     bias=eps_col[:],
                 )
+
+        def factors(j0, j1):
             nc.vector.tensor_tensor(
                 out=c_scale[:, j0:j1, :], in0=zn_psum[:, j0:j1, 0:N_B], in1=x_rstd[:, j0:j1, :], op=ALU.mult
             )
@@ -178,7 +180,8 @@ def tile_causalfeaturetransformer_pa_t_kernel(
         nc.scalar.activation(out=zn_sq[:], in_=zn_psum[:, :, 0:N_B], func=ACT.Square)
         centre(1)
         nc.vector.bn_aggr(out=tok_mv[:, 2, :], in_=tok_stats[:, 2, :])
-        scales_of_tiles(0, 2)
+        spreads(0, 2)
+        factors(0, 2)
         nc.vector.bn_stats(out=tok_stats[:, 3, :], in_=tokens[:, 3, :])
 
         w_grouped = [
@@ -246,49 +249,53 @@ def tile_causalfeaturetransformer_pa_t_kernel(
             else:
                 nc.scalar.activation(out=dst, in_=src, func=ACT.Identity, scale=c)
 
+        turned = {}
+
+        def new_row(n):
+            grouped_of[n] = work.tile([P, SEQ, PACK], BF16, name="grouped", align_bytes=64)
+
         def turn_words(n, j0, j1):
-            if j0 == 0:
-                grouped_of[n] = work.tile([P, SEQ, PACK], BF16, name="grouped", align_bytes=64)
             words_t = psum_t.tile([P, WORD_TILES, 2, P], F32, tag="t")
+            turned[n, j0] = words_t
             for j in range(j0, j1):
                 words = words_of[n][:, j, :].bitcast(F32)
                 for u in range(2):
                     nc.tensor.transpose(words_t[:, j - j0, u, :], words[:, u * P : (u + 1) * P], ident_f32[:])
+
+        def empty_words(n, j0, j1):
             nc.scalar.copy(
                 out=grouped_of[n][:, j0 * P : j1 * P, :]
                 .rearrange("q i t -> q (i t)")
                 .bitcast(F32)
                 .rearrange("q (j i u) -> q j i u", j=j1 - j0, u=2),
-                in_=words_t[:, 0 : j1 - j0, :, :].rearrange("q j u i -> q j i u"),
+                in_=turned[n, j0][:, 0 : j1 - j0, :, :].rearrange("q j u i -> q j i u"),
             )
 
-        def turn(n, tiles):
-            turned = {}
-            for j in tiles:
-                xn_t = psum_t.tile([P, PACK, P], F32, tag="t")
-                turned[j] = xn_t
-                for t in range(PACK):
-                    nc.tensor.matmul(
-                        out=xn_t[:, t, :],
-                        lhsT=z_of[n][:, j - WORD_TILES, t * P : (t + 1) * P],
-                        rhs=ident_f32[:],
-                        start=(t == 0),
-                        stop=False,
-                        is_transpose=True,
-                    )
-            for j in tiles:
+        def turn(n, j):
+            xn_t = psum_t.tile([P, PACK, P], F32, tag="t")
+            turned[n, j] = xn_t
+            for t in range(PACK):
                 nc.tensor.matmul(
-                    out=turned[j][:].rearrange("q t i -> q (t i)"),
-                    lhsT=shift_rows[:],
-                    rhs=picks[:].rearrange("k t i -> k (t i)"),
-                    start=False,
-                    stop=True,
+                    out=xn_t[:, t, :],
+                    lhsT=z_of[n][:, j - WORD_TILES, t * P : (t + 1) * P],
+                    rhs=ident_f32[:],
+                    start=(t == 0),
+                    stop=False,
+                    is_transpose=True,
                 )
-            for j in tiles:
-                nc.scalar.copy(
-                    out=grouped_of[n][:, j * P : (j + 1) * P, :].rearrange("q (c i) t -> q c t i", i=RUN),
-                    in_=turned[j][:].rearrange("q t (c i) -> q c t i", i=RUN),
-                )
+            nc.tensor.matmul(
+                out=xn_t[:].rearrange("q t i -> q (t i)"),
+                lhsT=shift_rows[:],
+                rhs=picks[:].rearrange("k t i -> k (t i)"),
+                start=False,
+                stop=True,
+            )
+
+        def empty(n, j):
+            nc.scalar.copy(
+                out=grouped_of[n][:, j * P : (j + 1) * P, :].rearrange("q (c i) t -> q c t i", i=RUN),
+                in_=turned[n, j][:].rearrange("q t (c i) -> q c t i", i=RUN),
+            )
 
         def quantise(n, j0, j1):
             if j0 == 0:
@@ -303,6 +310,11 @@ def tile_causalfeaturetransformer_pa_t_kernel(
                 scales=scales[:, cols],
                 in_=grouped_of[n][:, cols, :].rearrange("q w t -> q (w t)"),
             )
+
+        def gpsimd_biases(n):
+            if n == 0:
+                return ()
+            return LAST_ROW_BIASES if n == N_B - 1 else GPSIMD_BIASES
 
         def project(n, j, o):
             codes, scales = codes_of[n]
@@ -320,7 +332,7 @@ def tile_causalfeaturetransformer_pa_t_kernel(
                 stop=True,
             )
             dst = res_of[n][o][:, j, :]
-            if 2 * j + o in (LAST_ROW_BIASES if n == N_B - 1 else GPSIMD_BIASES):
+            if 2 * j + o in gpsimd_biases(n):
                 nc.scalar.copy(out=dst, in_=acc[:])
                 nc.gpsimd.tensor_tensor(out=dst, in0=dst, in1=bias_all[:, o, :], op=ALU.add)
             else:
@@ -330,78 +342,95 @@ def tile_causalfeaturetransformer_pa_t_kernel(
                     out=out_views[o][n][:, j - 1 : j + 1, :], in_=res_of[n][o][:, j - 1 : j + 1, :]
                 )
 
-        def project_pair(n, j):
-            for o in range(2):
-                project(n, j, o)
-
-        def scale_rest(n):
-            for j in range(WORD_TILES, TILES):
-                scale(n, j, "scalar")
-
-        def turn_row(n):
-            turn_words(n, 0, WORD_TILES)
-            turn(n, range(WORD_TILES, TILES))
+        def product(n, k):
+            project(n, k // 2, k % 2)
 
         half = D_EMB // 2
         regroup(0, 0, half, "gpsimd")
         regroup(0, half, D_EMB, "gpsimd")
         regroup(1, 0, half, "gpsimd")
         regroup(1, half, D_EMB, "scalar")
+        new_row(0)
         finish(0, 0)
-        turn_words(0, 0, 1)
         nc.vector.bn_aggr(out=tok_mv[:, 3, :], in_=tok_stats[:, 3, :])
+        spreads(2, TILES)
+        turn_words(0, 0, 1)
+        empty_words(0, 0, 1)
         finish(0, 1)
         turn_words(0, 1, 2)
-        scales_of_tiles(2, TILES)
+        empty_words(0, 1, 2)
         shift_product_operands()
+        factors(2, TILES)
         quantise_weight(0)
         quantise(0, 0, 1)
-        project(0, 0, 0)
         centre(2)
         scale(0, 2, "scalar")
-        quantise_weight(1)
+        quantise(0, 1, 2)
         centre(3)
         scale(0, 3, "gpsimd")
-        turn(0, (2,))
-        project(0, 0, 1)
-        quantise(0, 1, 2)
+        scale(1, 2, "scalar")
         finish(1, 0)
+        product(0, 0)
+        scale(1, 3, "gpsimd")
+        quantise_weight(1)
+        product(0, 2)
+        turn(0, 2)
+        empty(0, 2)
+        turn(0, 3)
+        empty(0, 3)
         finish(1, 1)
-        project_pair(0, 1)
-        turn(0, (3,))
-        turn_words(1, 0, WORD_TILES)
-        scale_rest(1)
-        quantise(0, 2, 4)
-        project_pair(0, 2)
-        turn(1, (2, 3))
-        scale_rest(2)
+        quantise(0, 2, 3)
+        product(0, 1)
+        quantise(0, 3, 4)
+        scale(2, 2, "scalar")
+        scale(2, 3, "gpsimd")
+        new_row(1)
+        turn_words(1, 0, 2)
+        turn(1, 2)
+        empty_words(1, 0, 2)
+        empty(1, 2)
+        product(0, 3)
         finish(2, 0)
-        project_pair(0, 3)
+        product(0, 4)
+        turn(1, 3)
+        empty(1, 3)
         finish(2, 1)
+        product(0, 5)
+        new_row(2)
+        turn_words(2, 0, 2)
+        turn(2, 2)
+        empty_words(2, 0, 2)
+        empty(2, 2)
+        product(0, 6)
         quantise(1, 0, TILES)
-        turn_row(2)
-        scale_rest(3)
-        finish(3, 0)
-        finish(3, 1)
+        product(0, 7)
+        turn(2, 3)
+        empty(2, 3)
+        scale(3, 2, "scalar")
+        scale(3, 3, "scalar")
 
         for n in range(1, N_B):
-            if 1 < n < N_B - 1:
+            ahead = n + 2 < N_B
+            if n + 1 < N_B:
                 quantise(n + 1, 0, TILES)
-            project_pair(n, 0)
-            project_pair(n, 1)
-            if n == 1:
-                quantise(2, 0, TILES)
-            if n + 3 < N_B:
-                finish(n + 3, 0)
-                finish(n + 3, 1)
-            if n + 2 < N_B:
-                turn_words(n + 2, 0, WORD_TILES)
-                turn(n + 2, (2,))
-            project_pair(n, 2)
-            if n + 2 < N_B:
+            for k in range(4):
+                product(n, k)
+            if ahead:
+                finish(n + 2, 0)
+                finish(n + 2, 1)
+                new_row(n + 2)
+                turn(n + 2, 2)
+                empty(n + 2, 2)
+            product(n, 4)
+            product(n, 5)
+            product(n, 6)
+            if ahead:
                 if n + 3 < N_B:
                     scale(n + 3, 2, "scalar")
-                turn(n + 2, (3,))
-            project_pair(n, 3)
+                turn(n + 2, 3)
+                turn_words(n + 2, 0, 2)
+                empty(n + 2, 3)
+                empty_words(n + 2, 0, 2)
+            product(n, 7)
             if n + 3 < N_B:
                 scale(n + 3, 3, "scalar")

@@ -41,8 +41,7 @@ def tile_causalfeaturetransformer_pa_t_kernel(
         work = ctx.enter_context(tc.tile_pool(name="work", bufs=2))
         results = ctx.enter_context(tc.tile_pool(name="results", bufs=3))
         psum_keep = ctx.enter_context(tc.psum_pool(name="psum_keep", bufs=1))
-        psum_t = ctx.enter_context(tc.psum_pool(name="psum_t", bufs=2))
-        psum_mx = ctx.enter_context(tc.psum_pool(name="psum_mx", bufs=5))
+        banks = ctx.enter_context(tc.psum_pool(name="banks", bufs=7))
 
         z_raw = keep.tile([N_B, D_FEAT], BF16)
         nc.sync.dma_start(out=z_raw[:], in_=Z)
@@ -91,7 +90,7 @@ def tile_causalfeaturetransformer_pa_t_kernel(
         nc.vector.memset(zn_rows[:], 0.0)
         nc.vector.memset(zn_rows[0:N_B, SEQ - 1 : SEQ], 1.0)
 
-        gain = psum_mx.tile([P, D_EMB], F32, name="acc")
+        gain = banks.tile([P, D_EMB], F32, name="bank")
         nc.tensor.matmul(out=gain[:], lhsT=ones[:], rhs=rows[:, 0, :], start=True, stop=True)
         shift_w = psum_keep.tile([P, 2, 2 * P], F32)
         for u in range(2):
@@ -131,7 +130,7 @@ def tile_causalfeaturetransformer_pa_t_kernel(
             )
         for j in range(2):
             nc.vector.bn_aggr(out=tok_mv[:, j, :], in_=tok_stats[:, j, :])
-        zn_psum = psum_t.tile([P, TILES, P], F32, tag="t")
+        zn_psum = banks.tile([P, TILES, P], F32, name="bank")
         for j in range(TILES):
             nc.tensor.transpose(zn_psum[:, j, :], zn_rows[:, j * P : (j + 1) * P], ident_f32[:])
 
@@ -214,7 +213,7 @@ def tile_causalfeaturetransformer_pa_t_kernel(
         )
 
         def shift_product_operands():
-            shift_psum = psum_t.tile([P, P], BF16, tag="t")
+            shift_psum = banks.tile([P, P], BF16, name="bank")
             nc.tensor.transpose(shift_psum[:], shift_cols[:], ident_bf16[:])
             nc.scalar.copy(out=shift_rows[:], in_=shift_psum[:])
 
@@ -237,7 +236,7 @@ def tile_causalfeaturetransformer_pa_t_kernel(
             )
 
         def scale(n, j, engine):
-            if j == WORD_TILES:
+            if n not in z_of:
                 z_of[n] = work.tile([P, TILES - WORD_TILES, D_EMB], F32, name="z", bufs=3)
             dst = z_of[n][:, j - WORD_TILES, :]
             src = centred[:, j - WORD_TILES, :, :].rearrange("p t q -> p (t q)")
@@ -255,7 +254,7 @@ def tile_causalfeaturetransformer_pa_t_kernel(
             grouped_of[n] = work.tile([P, SEQ, PACK], BF16, name="grouped", align_bytes=64)
 
         def turn_words(n, j0, j1):
-            words_t = psum_t.tile([P, WORD_TILES, 2, P], F32, tag="t")
+            words_t = banks.tile([P, WORD_TILES, 2, P], F32, name="bank")
             turned[n, j0] = words_t
             for j in range(j0, j1):
                 words = words_of[n][:, j, :].bitcast(F32)
@@ -272,7 +271,7 @@ def tile_causalfeaturetransformer_pa_t_kernel(
             )
 
         def turn(n, j):
-            xn_t = psum_t.tile([P, PACK, P], F32, tag="t")
+            xn_t = banks.tile([P, PACK, P], F32, name="bank")
             turned[n, j] = xn_t
             for t in range(PACK):
                 nc.tensor.matmul(
@@ -313,7 +312,7 @@ def tile_causalfeaturetransformer_pa_t_kernel(
 
         def gpsimd_biases(n):
             if n == 0:
-                return ()
+                return (1, 3)
             return LAST_ROW_BIASES if n == N_B - 1 else GPSIMD_BIASES
 
         def project(n, j, o):
@@ -321,7 +320,7 @@ def tile_causalfeaturetransformer_pa_t_kernel(
             if j == 0 and o == 0:
                 res_of[n] = [results.tile([P, TILES, D_EMB], F32, name="res%d" % k) for k in range(2)]
             cols = slice(j * P, (j + 1) * P)
-            acc = psum_mx.tile([P, D_EMB], F32, name="acc")
+            acc = banks.tile([P, D_EMB], F32, name="bank")
             nc.tensor.matmul_mx(
                 out=acc[:],
                 lhsT=codes[:, cols].bitcast(FP8X4),
@@ -337,10 +336,10 @@ def tile_causalfeaturetransformer_pa_t_kernel(
                 nc.gpsimd.tensor_tensor(out=dst, in0=dst, in1=bias_all[:, o, :], op=ALU.add)
             else:
                 nc.vector.tensor_tensor(out=dst, in0=acc[:], in1=bias_all[:, o, :], op=ALU.add)
-            if j % 2 == 1:
-                nc.sync.dma_start(
-                    out=out_views[o][n][:, j - 1 : j + 1, :], in_=res_of[n][o][:, j - 1 : j + 1, :]
-                )
+            tiles = 1 if n == 0 else 2
+            if j % tiles == tiles - 1:
+                part = slice(j + 1 - tiles, j + 1)
+                nc.sync.dma_start(out=out_views[o][n][:, part, :], in_=res_of[n][o][:, part, :])
 
         def product(n, k):
             project(n, k // 2, k % 2)
@@ -352,61 +351,60 @@ def tile_causalfeaturetransformer_pa_t_kernel(
         regroup(1, half, D_EMB, "scalar")
         new_row(0)
         finish(0, 0)
+        turn_words(0, 0, 1)
+        finish(0, 1)
         nc.vector.bn_aggr(out=tok_mv[:, 3, :], in_=tok_stats[:, 3, :])
         spreads(2, TILES)
-        turn_words(0, 0, 1)
-        empty_words(0, 0, 1)
-        finish(0, 1)
-        turn_words(0, 1, 2)
-        empty_words(0, 1, 2)
-        shift_product_operands()
-        factors(2, TILES)
-        quantise_weight(0)
-        quantise(0, 0, 1)
         centre(2)
+        empty_words(0, 0, 1)
+        turn_words(0, 1, 2)
+        factors(2, TILES)
+        empty_words(0, 1, 2)
         scale(0, 2, "scalar")
-        quantise(0, 1, 2)
         centre(3)
         scale(0, 3, "gpsimd")
-        scale(1, 2, "scalar")
+        quantise_weight(0)
+        quantise(0, 0, 1)
         finish(1, 0)
-        product(0, 0)
-        scale(1, 3, "gpsimd")
-        quantise_weight(1)
-        product(0, 2)
+        shift_product_operands()
+        quantise(0, 1, 2)
         turn(0, 2)
+        scale(1, 2, "scalar")
+        quantise_weight(1)
+        product(0, 0)
         empty(0, 2)
+        finish(1, 1)
+        scale(1, 3, "gpsimd")
         turn(0, 3)
         empty(0, 3)
-        finish(1, 1)
-        quantise(0, 2, 3)
-        product(0, 1)
-        quantise(0, 3, 4)
         scale(2, 2, "scalar")
         scale(2, 3, "gpsimd")
+        product(0, 2)
+        finish(2, 0)
+        product(0, 1)
         new_row(1)
         turn_words(1, 0, 2)
-        turn(1, 2)
         empty_words(1, 0, 2)
-        empty(1, 2)
+        quantise(0, 2, 4)
+        turn(1, 2)
         product(0, 3)
-        finish(2, 0)
-        product(0, 4)
-        turn(1, 3)
-        empty(1, 3)
-        finish(2, 1)
-        product(0, 5)
         new_row(2)
+        finish(2, 1)
+        empty(1, 2)
+        turn(1, 3)
+        product(0, 4)
+        product(0, 5)
+        empty(1, 3)
+        product(0, 6)
         turn_words(2, 0, 2)
         turn(2, 2)
-        empty_words(2, 0, 2)
-        empty(2, 2)
-        product(0, 6)
         quantise(1, 0, TILES)
         product(0, 7)
+        empty_words(2, 0, 2)
+        scale(3, 2, "scalar")
+        empty(2, 2)
         turn(2, 3)
         empty(2, 3)
-        scale(3, 2, "scalar")
         scale(3, 3, "scalar")
 
         for n in range(1, N_B):

@@ -21,7 +21,7 @@ D_EMB = 512
 TILES = SEQ // P
 EPS = 1e-5
 WORD_TILES = 2
-GPSIMD_BIASES = (0, 1, 3)
+GPSIMD_BIASES = (0, 3, 5)
 LAST_ROW_BIASES = (0, 1)
 
 FLOPS = 2 * N_B * SEQ * D_EMB * (2 * D_EMB)
@@ -90,6 +90,38 @@ def tile_causalfeaturetransformer_pa_t_kernel(
         nc.vector.memset(zn_rows[:], 0.0)
         nc.vector.memset(zn_rows[0:N_B, SEQ - 1 : SEQ], 1.0)
 
+        tok_stats = keep.tile([P, TILES, 6], F32)
+        tok_mv = keep.tile([P, TILES, 2], F32)
+        z_stats = keep.tile([N_B, 6], F32)
+        nc.vector.bn_stats(out=z_stats[:], in_=z_raw[:])
+        z_mv = keep.tile([N_B, 2], F32)
+        nc.vector.bn_aggr(out=z_mv[:], in_=z_stats[:])
+        nc.vector.bn_stats(out=tok_stats[:, 0, :], in_=tokens[:, 0, :])
+        z_rstd = keep.tile([N_B, 1], F32)
+        nc.scalar.activation(
+            out=z_rstd[:], in_=z_mv[:, 1:2], func=ACT.Abs_reciprocal_sqrt, bias=eps_col[0:N_B, :]
+        )
+        zn_view = zn_rows[0:N_B, :].rearrange("n (j p) -> n j p", j=TILES)
+        full = (P - 1) * TILES
+        for dst, cols in (
+            (zn_view[:, 0 : TILES - 1, P - 1 : P], slice(full, D_FEAT)),
+            (zn_view[:, :, 0 : P - 1], slice(0, full)),
+        ):
+            nc.vector.tensor_scalar(
+                out=dst,
+                in0=z_raw[:, cols].rearrange("n (p j) -> n j p", j=dst.shape[1]),
+                scalar1=z_mv[:, 0:1],
+                scalar2=z_rstd[:],
+                op0=ALU.subtract,
+                op1=ALU.mult,
+            )
+        nc.vector.bn_stats(out=tok_stats[:, 1, :], in_=tokens[:, 1, :])
+        for j in range(2):
+            nc.vector.bn_aggr(out=tok_mv[:, j, :], in_=tok_stats[:, j, :])
+        zn_psum = banks.tile([P, TILES, P], F32, name="bank")
+        for j in range(TILES):
+            nc.tensor.transpose(zn_psum[:, j, :], zn_rows[:, j * P : (j + 1) * P], ident_f32[:])
+
         gain = banks.tile([P, D_EMB], F32, name="bank")
         nc.tensor.matmul(out=gain[:], lhsT=ones[:], rhs=rows[:, 0, :], start=True, stop=True)
         shift_w = psum_keep.tile([P, 2, 2 * P], F32)
@@ -101,38 +133,6 @@ def tile_causalfeaturetransformer_pa_t_kernel(
                 start=True,
                 stop=True,
             )
-
-        tok_stats = keep.tile([P, TILES, 6], F32)
-        tok_mv = keep.tile([P, TILES, 2], F32)
-        z_stats = keep.tile([N_B, 6], F32)
-        nc.vector.bn_stats(out=z_stats[:], in_=z_raw[:])
-        nc.vector.bn_stats(out=tok_stats[:, 0, :], in_=tokens[:, 0, :])
-        z_mv = keep.tile([N_B, 2], F32)
-        nc.vector.bn_aggr(out=z_mv[:], in_=z_stats[:])
-        z_rstd = keep.tile([N_B, 1], F32)
-        nc.scalar.activation(
-            out=z_rstd[:], in_=z_mv[:, 1:2], func=ACT.Abs_reciprocal_sqrt, bias=eps_col[0:N_B, :]
-        )
-        nc.vector.bn_stats(out=tok_stats[:, 1, :], in_=tokens[:, 1, :])
-        zn_view = zn_rows[0:N_B, :].rearrange("n (j p) -> n j p", j=TILES)
-        full = (P - 1) * TILES
-        for dst, cols in (
-            (zn_view[:, :, 0 : P - 1], slice(0, full)),
-            (zn_view[:, 0 : TILES - 1, P - 1 : P], slice(full, D_FEAT)),
-        ):
-            nc.vector.tensor_scalar(
-                out=dst,
-                in0=z_raw[:, cols].rearrange("n (p j) -> n j p", j=dst.shape[1]),
-                scalar1=z_mv[:, 0:1],
-                scalar2=z_rstd[:],
-                op0=ALU.subtract,
-                op1=ALU.mult,
-            )
-        for j in range(2):
-            nc.vector.bn_aggr(out=tok_mv[:, j, :], in_=tok_stats[:, j, :])
-        zn_psum = banks.tile([P, TILES, P], F32, name="bank")
-        for j in range(TILES):
-            nc.tensor.transpose(zn_psum[:, j, :], zn_rows[:, j * P : (j + 1) * P], ident_f32[:])
 
         centred_w = keep.tile([P, WORD_TILES, 2, P, 2], F32)
         centred = keep.tile([P, TILES - WORD_TILES, PACK, P], F32)
@@ -174,14 +174,13 @@ def tile_causalfeaturetransformer_pa_t_kernel(
                 out=c_scale[:, j0:j1, :], in0=zn_psum[:, j0:j1, 0:N_B], in1=x_rstd[:, j0:j1, :], op=ALU.mult
             )
 
+        nc.scalar.activation(out=zn_sq[:], in_=zn_psum[:, :, 0:N_B], func=ACT.Square)
+        spreads(0, 2)
         nc.vector.bn_stats(out=tok_stats[:, 2, :], in_=tokens[:, 2, :])
         centre(0)
-        nc.scalar.activation(out=zn_sq[:], in_=zn_psum[:, :, 0:N_B], func=ACT.Square)
+        factors(0, 2)
         centre(1)
         nc.vector.bn_aggr(out=tok_mv[:, 2, :], in_=tok_stats[:, 2, :])
-        spreads(0, 2)
-        factors(0, 2)
-        nc.vector.bn_stats(out=tok_stats[:, 3, :], in_=tokens[:, 3, :])
 
         w_grouped = [
             keep.tile([P, D_EMB, PACK], BF16, name="w_grouped%d" % o, align_bytes=64) for o in range(2)
@@ -345,67 +344,68 @@ def tile_causalfeaturetransformer_pa_t_kernel(
             project(n, k // 2, k % 2)
 
         half = D_EMB // 2
+        new_row(0)
         regroup(0, 0, half, "gpsimd")
-        regroup(0, half, D_EMB, "gpsimd")
+        regroup(0, half, D_EMB, "scalar")
         regroup(1, 0, half, "gpsimd")
         regroup(1, half, D_EMB, "scalar")
-        new_row(0)
+        nc.vector.bn_stats(out=tok_stats[:, 3, :], in_=tokens[:, 3, :])
         finish(0, 0)
-        turn_words(0, 0, 1)
-        finish(0, 1)
         nc.vector.bn_aggr(out=tok_mv[:, 3, :], in_=tok_stats[:, 3, :])
         spreads(2, TILES)
-        centre(2)
+        shift_product_operands()
+        turn_words(0, 0, 1)
         empty_words(0, 0, 1)
+        centre(2)
+        finish(0, 1)
         turn_words(0, 1, 2)
         factors(2, TILES)
-        empty_words(0, 1, 2)
         scale(0, 2, "scalar")
         centre(3)
-        scale(0, 3, "gpsimd")
-        quantise_weight(0)
-        quantise(0, 0, 1)
-        finish(1, 0)
-        shift_product_operands()
-        quantise(0, 1, 2)
-        turn(0, 2)
-        scale(1, 2, "scalar")
-        quantise_weight(1)
-        product(0, 0)
-        empty(0, 2)
-        finish(1, 1)
+        scale(0, 3, "scalar")
         scale(1, 3, "gpsimd")
+        scale(2, 3, "gpsimd")
+        finish(1, 0)
+        empty_words(0, 1, 2)
+        turn(0, 2)
+        empty(0, 2)
+        quantise(0, 0, 1)
+        quantise_weight(0)
         turn(0, 3)
         empty(0, 3)
+        quantise(0, 1, 2)
+        scale(1, 2, "gpsimd")
         scale(2, 2, "scalar")
-        scale(2, 3, "gpsimd")
+        quantise_weight(1)
+        finish(1, 1)
+        product(0, 0)
+        quantise(0, 2, 4)
         product(0, 2)
-        finish(2, 0)
         product(0, 1)
+        product(0, 3)
         new_row(1)
         turn_words(1, 0, 2)
         empty_words(1, 0, 2)
-        quantise(0, 2, 4)
         turn(1, 2)
-        product(0, 3)
-        new_row(2)
-        finish(2, 1)
         empty(1, 2)
-        turn(1, 3)
+        finish(2, 0)
+        finish(2, 1)
         product(0, 4)
         product(0, 5)
+        turn(1, 3)
         empty(1, 3)
+        scale(3, 2, "gpsimd")
+        scale(3, 3, "gpsimd")
         product(0, 6)
-        turn_words(2, 0, 2)
-        turn(2, 2)
         quantise(1, 0, TILES)
-        product(0, 7)
-        empty_words(2, 0, 2)
-        scale(3, 2, "scalar")
+        new_row(2)
+        turn(2, 2)
+        turn_words(2, 0, 2)
         empty(2, 2)
+        empty_words(2, 0, 2)
         turn(2, 3)
+        product(0, 7)
         empty(2, 3)
-        scale(3, 3, "scalar")
 
         for n in range(1, N_B):
             ahead = n + 2 < N_B

@@ -21,7 +21,7 @@ D_EMB = 512
 TILES = SEQ // P
 EPS = 1e-5
 WORD_TILES = 2
-GPSIMD_BIASES = (0, 3, 5)
+GPSIMD_BIASES = (1, 3, 5)
 LAST_ROW_BIASES = (0, 1)
 
 FLOPS = 2 * N_B * SEQ * D_EMB * (2 * D_EMB)
@@ -409,10 +409,10 @@ def tile_causalfeaturetransformer_pa_t_kernel(
 
         for n in range(1, N_B):
             ahead = n + 2 < N_B
-            if n + 1 < N_B:
-                quantise(n + 1, 0, TILES)
             for k in range(4):
                 product(n, k)
+                if k == 0 and n + 1 < N_B:
+                    quantise(n + 1, 0, TILES)
             if ahead:
                 finish(n + 2, 0)
                 finish(n + 2, 1)

from contextlib import ExitStack

import concourse.mybir as mybir
from concourse.masks import make_identity

F32 = mybir.dt.float32
BF16 = mybir.dt.bfloat16
U32 = mybir.dt.uint32
U8 = mybir.dt.uint8
FP8X4 = mybir.dt.float8_e4m3fn_x4
ALU = mybir.AluOpType
ACT = mybir.ActivationFunctionType

P = 128
PACK = 4
RUN = 4
N_B = 16
D_FEAT = 511
SEQ = 512
D_EMB = 512
TILES = SEQ // P
EPS = 1e-5
WORD_TILES = 2
GPSIMD_BIASES = (1, 3, 5)
LAST_ROW_BIASES = (0, 1)

FLOPS = 2 * N_B * SEQ * D_EMB * (2 * D_EMB)


def tile_causalfeaturetransformer_pa_t_kernel(
    tc, Z, feat_emb, label_token, g1, be1, wk, bk, wv, bv, out_0, out_1
):
    nc = tc.nc
    weights = (wk, wv)
    biases = (bk, bv)
    out_views = tuple(o.rearrange("n (p j) e -> n p j e", j=TILES) for o in (out_0, out_1))

    with ExitStack() as ctx:
        ctx.enter_context(tc.manual_schedule())
        keep = ctx.enter_context(tc.tile_pool(name="keep", bufs=1))
        work = ctx.enter_context(tc.tile_pool(name="work", bufs=2))
        results = ctx.enter_context(tc.tile_pool(name="results", bufs=3))
        psum_keep = ctx.enter_context(tc.psum_pool(name="psum_keep", bufs=1))
        banks = ctx.enter_context(tc.psum_pool(name="banks", bufs=7))

        z_raw = keep.tile([N_B, D_FEAT], BF16)
        nc.sync.dma_start(out=z_raw[:], in_=Z)
        tokens = keep.tile([P, TILES, D_EMB], BF16)

        def load_tokens(j, p0, p1):
            nc.sync.dma_start(
                out=tokens[p0:p1, j, :], in_=feat_emb[p0 * TILES + j : (p1 - 1) * TILES + j + 1 : TILES]
            )

        rows = keep.tile([P, 2, D_EMB], BF16)
        nc.vector.memset(rows[:], 0.0)
        load_tokens(0, 0, P)
        load_tokens(1, 0, P)
        nc.scalar.dma_start(out=rows[0:1, 0, :], in_=g1.rearrange("(o d) -> o d", o=1))
        load_tokens(2, 0, P)
        load_tokens(3, 0, P // 2)
        w_raw = [keep.tile([P, PACK, D_EMB], BF16, name="w_raw%d" % o) for o in range(2)]
        nc.sync.dma_start(out=w_raw[0][:], in_=weights[0].rearrange("(q t) e -> q t e", t=PACK))
        nc.scalar.dma_start(out=rows[0:1, 1, :], in_=be1.rearrange("(o d) -> o d", o=1))
        load_tokens(3, P // 2, P - 1)
        nc.sync.dma_start(out=tokens[P - 1 : P, 3:4, :], in_=label_token)
        nc.sync.dma_start(out=w_raw[1][:], in_=weights[1].rearrange("(q t) e -> q t e", t=PACK))
        shift_cols = keep.tile([P, P], BF16)
        nc.vector.memset(shift_cols[:], 0.0)
        nc.sync.dma_start(out=shift_cols[:, 0:PACK], in_=be1.rearrange("(q t) -> q t", t=PACK))
        bias_all = keep.tile([P, 2, D_EMB], BF16)
        for o in range(2):
            nc.sync.dma_start(out=bias_all[:, o, :], in_=biases[o].partition_broadcast(P))

        one_col = keep.tile([P, 1], F32)
        nc.vector.memset(one_col[:], 1.0)
        warm = keep.tile([P, 1], F32)
        nc.scalar.activation(out=warm[:], in_=one_col[:], func=ACT.Abs_reciprocal_sqrt)
        eps_col = keep.tile([P, 1], F32)
        nc.vector.tensor_scalar(
            out=eps_col[:], in0=one_col[:], scalar1=0.0, scalar2=EPS, op0=ALU.mult, op1=ALU.add
        )
        ones = keep.tile([P, P], BF16)
        nc.vector.memset(ones[:], 1.0)
        ident_f32 = keep.tile([P, P], F32)
        make_identity(nc, ident_f32[:])
        ident_bf16 = keep.tile([P, P], BF16)
        make_identity(nc, ident_bf16[:])
        zn_rows = keep.tile([P, SEQ], F32)
        nc.vector.memset(zn_rows[:], 0.0)
        nc.vector.memset(zn_rows[0:N_B, SEQ - 1 : SEQ], 1.0)

        tok_stats = keep.tile([P, TILES, 6], F32)
        tok_mv = keep.tile([P, TILES, 2], F32)
        z_stats = keep.tile([N_B, 6], F32)
        nc.vector.bn_stats(out=z_stats[:], in_=z_raw[:])
        z_mv = keep.tile([N_B, 2], F32)
        nc.vector.bn_aggr(out=z_mv[:], in_=z_stats[:])
        nc.vector.bn_stats(out=tok_stats[:, 0, :], in_=tokens[:, 0, :])
        z_rstd = keep.tile([N_B, 1], F32)
        nc.scalar.activation(
            out=z_rstd[:], in_=z_mv[:, 1:2], func=ACT.Abs_reciprocal_sqrt, bias=eps_col[0:N_B, :]
        )
        zn_view = zn_rows[0:N_B, :].rearrange("n (j p) -> n j p", j=TILES)
        full = (P - 1) * TILES
        for dst, cols in (
            (zn_view[:, 0 : TILES - 1, P - 1 : P], slice(full, D_FEAT)),
            (zn_view[:, :, 0 : P - 1], slice(0, full)),
        ):
            nc.vector.tensor_scalar(
                out=dst,
                in0=z_raw[:, cols].rearrange("n (p j) -> n j p", j=dst.shape[1]),
                scalar1=z_mv[:, 0:1],
                scalar2=z_rstd[:],
                op0=ALU.subtract,
                op1=ALU.mult,
            )
        nc.vector.bn_stats(out=tok_stats[:, 1, :], in_=tokens[:, 1, :])
        for j in range(2):
            nc.vector.bn_aggr(out=tok_mv[:, j, :], in_=tok_stats[:, j, :])
        zn_psum = banks.tile([P, TILES, P], F32, name="bank")
        for j in range(TILES):
            nc.tensor.transpose(zn_psum[:, j, :], zn_rows[:, j * P : (j + 1) * P], ident_f32[:])

        gain = banks.tile([P, D_EMB], F32, name="bank")
        nc.tensor.matmul(out=gain[:], lhsT=ones[:], rhs=rows[:, 0, :], start=True, stop=True)
        shift_w = psum_keep.tile([P, 2, 2 * P], F32)
        for u in range(2):
            nc.tensor.matmul(
                out=shift_w[:, u, :],
                lhsT=ones[:],
                rhs=rows[:, 1, :].rearrange("k (q u e) -> k u q e", u=2, e=2)[:, u, :, :],
                start=True,
                stop=True,
            )

        centred_w = keep.tile([P, WORD_TILES, 2, P, 2], F32)
        centred = keep.tile([P, TILES - WORD_TILES, PACK, P], F32)

        def centre(j):
            if j < WORD_TILES:
                parts = [
                    (centred_w[:, j, u, :, :], "p (q u e) -> p u q e", {"u": 2, "e": 2}, u) for u in range(2)
                ]
            else:
                parts = [(centred[:, j - WORD_TILES, :, :], "p (o q t) -> p o t q", {"o": 1, "t": PACK}, 0)]
            for dst, order, sizes, i in parts:
                nc.vector.scalar_tensor_tensor(
                    out=dst,
                    in0=tokens[:, j, :].rearrange(order, **sizes)[:, i, :, :],
                    scalar=tok_mv[:, j, 0:1],
                    in1=gain[:].rearrange(order, **sizes)[:, i, :, :],
                    op0=ALU.subtract,
                    op1=ALU.mult,
                )

        shape_c = [P, TILES, N_B]
        zn_sq = keep.tile(shape_c, F32)
        x_rstd = keep.tile(shape_c, F32)
        c_scale = keep.tile(shape_c, F32)

        def spreads(j0, j1):
            for j in range(j0, j1):
                nc.scalar.activation(
                    out=x_rstd[:, j, :],
                    in_=zn_sq[:, j, :],
                    func=ACT.Abs_reciprocal_sqrt,
                    scale=tok_mv[:, j, 1:2],
                    bias=eps_col[:],
                )

        def factors(j0, j1):
            nc.vector.tensor_tensor(
                out=c_scale[:, j0:j1, :], in0=zn_psum[:, j0:j1, 0:N_B], in1=x_rstd[:, j0:j1, :], op=ALU.mult
            )

        nc.scalar.activation(out=zn_sq[:], in_=zn_psum[:, :, 0:N_B], func=ACT.Square)
        spreads(0, 2)
        nc.vector.bn_stats(out=tok_stats[:, 2, :], in_=tokens[:, 2, :])
        centre(0)
        factors(0, 2)
        centre(1)
        nc.vector.bn_aggr(out=tok_mv[:, 2, :], in_=tok_stats[:, 2, :])

        w_grouped = [
            keep.tile([P, D_EMB, PACK], BF16, name="w_grouped%d" % o, align_bytes=64) for o in range(2)
        ]
        w_codes = [keep.tile([P, D_EMB], U32, name="w_codes%d" % o, align_bytes=64) for o in range(2)]
        w_scales = [keep.tile([P, D_EMB], U8, name="w_scales%d" % o, align_bytes=64) for o in range(2)]

        def regroup(o, e0, e1, engine):
            dst = w_grouped[o][:, e0:e1, :]
            src = w_raw[o][:, :, e0:e1].rearrange("q t e -> q e t")
            if engine == "scalar":
                nc.scalar.copy(out=dst, in_=src)
            elif engine == "vector":
                nc.vector.tensor_copy(out=dst, in_=src)
            else:
                nc.gpsimd.tensor_scalar(out=dst, in0=src, scalar1=1.0, scalar2=0.0, op0=ALU.mult, op1=ALU.add)

        def quantise_weight(o):
            nc.vector.quantize_mx(
                out=w_codes[o][:].bitcast(FP8X4),
                scales=w_scales[o][:],
                in_=w_grouped[o][:].rearrange("q e t -> q (e t)"),
            )

        shift_rows = keep.tile([P, P], BF16)
        picks = keep.tile([P, PACK, P], BF16)
        nc.scalar.copy(
            out=picks[:], in_=ident_bf16[:, 0:PACK].unsqueeze(2).to_broadcast([P, PACK, P])
        )

        def shift_product_operands():
            shift_psum = banks.tile([P, P], BF16, name="bank")
            nc.tensor.transpose(shift_psum[:], shift_cols[:], ident_bf16[:])
            nc.scalar.copy(out=shift_rows[:], in_=shift_psum[:])

        z_of = {}
        words_of = {}
        grouped_of = {}
        codes_of = {}
        res_of = {}

        def finish(n, j):
            if j == 0:
                words_of[n] = work.tile([P, WORD_TILES, D_EMB], BF16, name="words", align_bytes=64, bufs=6)
            nc.vector.scalar_tensor_tensor(
                out=words_of[n][:, j, :],
                in0=centred_w[:, j, :, :, :].rearrange("p u q e -> p (u q e)"),
                scalar=c_scale[:, j, n : n + 1],
                in1=shift_w[:].rearrange("p u w -> p (u w)"),
                op0=ALU.mult,
                op1=ALU.add,
            )

        def scale(n, j, engine):
            if n not in z_of:
                z_of[n] = work.tile([P, TILES - WORD_TILES, D_EMB], F32, name="z", bufs=3)
            dst = z_of[n][:, j - WORD_TILES, :]
            src = centred[:, j - WORD_TILES, :, :].rearrange("p t q -> p (t q)")
            c = c_scale[:, j, n : n + 1]
            if engine == "gpsimd":
                nc.gpsimd.tensor_scalar(
                    out=dst, in0=src, scalar1=c, scalar2=0.0, op0=ALU.mult, op1=ALU.add
                )
            else:
                nc.scalar.activation(out=dst, in_=src, func=ACT.Identity, scale=c)

        turned = {}

        def new_row(n):
            grouped_of[n] = work.tile([P, SEQ, PACK], BF16, name="grouped", align_bytes=64)

        def turn_words(n, j0, j1):
            words_t = banks.tile([P, WORD_TILES, 2, P], F32, name="bank")
            turned[n, j0] = words_t
            for j in range(j0, j1):
                words = words_of[n][:, j, :].bitcast(F32)
                for u in range(2):
                    nc.tensor.transpose(words_t[:, j - j0, u, :], words[:, u * P : (u + 1) * P], ident_f32[:])

        def empty_words(n, j0, j1):
            nc.scalar.copy(
                out=grouped_of[n][:, j0 * P : j1 * P, :]
                .rearrange("q i t -> q (i t)")
                .bitcast(F32)
                .rearrange("q (j i u) -> q j i u", j=j1 - j0, u=2),
                in_=turned[n, j0][:, 0 : j1 - j0, :, :].rearrange("q j u i -> q j i u"),
            )

        def turn(n, j):
            xn_t = banks.tile([P, PACK, P], F32, name="bank")
            turned[n, j] = xn_t
            for t in range(PACK):
                nc.tensor.matmul(
                    out=xn_t[:, t, :],
                    lhsT=z_of[n][:, j - WORD_TILES, t * P : (t + 1) * P],
                    rhs=ident_f32[:],
                    start=(t == 0),
                    stop=False,
                    is_transpose=True,
                )
            nc.tensor.matmul(
                out=xn_t[:].rearrange("q t i -> q (t i)"),
                lhsT=shift_rows[:],
                rhs=picks[:].rearrange("k t i -> k (t i)"),
                start=False,
                stop=True,
            )

        def empty(n, j):
            nc.scalar.copy(
                out=grouped_of[n][:, j * P : (j + 1) * P, :].rearrange("q (c i) t -> q c t i", i=RUN),
                in_=turned[n, j][:].rearrange("q t (c i) -> q c t i", i=RUN),
            )

        def quantise(n, j0, j1):
            if j0 == 0:
                codes_of[n] = (
                    work.tile([P, SEQ], U32, name="codes", align_bytes=64),
                    work.tile([P, SEQ], U8, name="scales", align_bytes=64),
                )
            codes, scales = codes_of[n]
            cols = slice(j0 * P, j1 * P)
            nc.vector.quantize_mx(
                out=codes[:, cols].bitcast(FP8X4),
                scales=scales[:, cols],
                in_=grouped_of[n][:, cols, :].rearrange("q w t -> q (w t)"),
            )

        def gpsimd_biases(n):
            if n == 0:
                return (1, 3)
            return LAST_ROW_BIASES if n == N_B - 1 else GPSIMD_BIASES

        def project(n, j, o):
            codes, scales = codes_of[n]
            if j == 0 and o == 0:
                res_of[n] = [results.tile([P, TILES, D_EMB], F32, name="res%d" % k) for k in range(2)]
            cols = slice(j * P, (j + 1) * P)
            acc = banks.tile([P, D_EMB], F32, name="bank")
            nc.tensor.matmul_mx(
                out=acc[:],
                lhsT=codes[:, cols].bitcast(FP8X4),
                lhsT_scale=scales[:, cols],
                rhs=w_codes[o][:].bitcast(FP8X4),
                rhs_scale=w_scales[o][:],
                start=True,
                stop=True,
            )
            dst = res_of[n][o][:, j, :]
            if 2 * j + o in gpsimd_biases(n):
                nc.scalar.copy(out=dst, in_=acc[:])
                nc.gpsimd.tensor_tensor(out=dst, in0=dst, in1=bias_all[:, o, :], op=ALU.add)
            else:
                nc.vector.tensor_tensor(out=dst, in0=acc[:], in1=bias_all[:, o, :], op=ALU.add)
            tiles = 1 if n == 0 else 2
            if j % tiles == tiles - 1:
                part = slice(j + 1 - tiles, j + 1)
                nc.sync.dma_start(out=out_views[o][n][:, part, :], in_=res_of[n][o][:, part, :])

        def product(n, k):
            project(n, k // 2, k % 2)

        half = D_EMB // 2
        new_row(0)
        regroup(0, 0, half, "gpsimd")
        regroup(0, half, D_EMB, "scalar")
        regroup(1, 0, half, "gpsimd")
        regroup(1, half, D_EMB, "scalar")
        nc.vector.bn_stats(out=tok_stats[:, 3, :], in_=tokens[:, 3, :])
        finish(0, 0)
        nc.vector.bn_aggr(out=tok_mv[:, 3, :], in_=tok_stats[:, 3, :])
        spreads(2, TILES)
        shift_product_operands()
        turn_words(0, 0, 1)
        empty_words(0, 0, 1)
        centre(2)
        finish(0, 1)
        turn_words(0, 1, 2)
        factors(2, TILES)
        scale(0, 2, "scalar")
        centre(3)
        scale(0, 3, "scalar")
        scale(1, 3, "gpsimd")
        scale(2, 3, "gpsimd")
        finish(1, 0)
        empty_words(0, 1, 2)
        turn(0, 2)
        empty(0, 2)
        quantise(0, 0, 1)
        quantise_weight(0)
        turn(0, 3)
        empty(0, 3)
        quantise(0, 1, 2)
        scale(1, 2, "gpsimd")
        scale(2, 2, "scalar")
        quantise_weight(1)
        finish(1, 1)
        product(0, 0)
        quantise(0, 2, 4)
        product(0, 2)
        product(0, 1)
        product(0, 3)
        new_row(1)
        turn_words(1, 0, 2)
        empty_words(1, 0, 2)
        turn(1, 2)
        empty(1, 2)
        finish(2, 0)
        finish(2, 1)
        product(0, 4)
        product(0, 5)
        turn(1, 3)
        empty(1, 3)
        scale(3, 2, "gpsimd")
        scale(3, 3, "gpsimd")
        product(0, 6)
        quantise(1, 0, TILES)
        new_row(2)
        turn(2, 2)
        turn_words(2, 0, 2)
        empty(2, 2)
        empty_words(2, 0, 2)
        turn(2, 3)
        product(0, 7)
        empty(2, 3)

        for n in range(1, N_B):
            ahead = n + 2 < N_B
            for k in range(4):
                product(n, k)
                if k == 0 and n + 1 < N_B:
                    quantise(n + 1, 0, TILES)
            if ahead:
                finish(n + 2, 0)
                finish(n + 2, 1)
                new_row(n + 2)
                turn(n + 2, 2)
                empty(n + 2, 2)
            product(n, 4)
            product(n, 5)
            product(n, 6)
            if ahead:
                if n + 3 < N_B:
                    scale(n + 3, 2, "scalar")
                turn(n + 2, 3)
                turn_words(n + 2, 0, 2)
                empty(n + 2, 3)
                empty_words(n + 2, 0, 2)
            product(n, 7)
            if n + 3 < N_B:
                scale(n + 3, 3, "scalar")
